import numpy as np
import ml_dtypes


def mxq(x, axis, fmt="e4m3"):
    dtype, down = {"e4m3": (ml_dtypes.float8_e4m3fn, 7), "e5m2": (ml_dtypes.float8_e5m2, 14)}[fmt]
    v = np.moveaxis(np.asarray(x, np.float32).astype(ml_dtypes.bfloat16).astype(np.float64), axis, -1)
    blocks = v.reshape(v.shape[:-1] + (-1, 32))
    amax = np.abs(blocks).max(-1, keepdims=True)
    byte = np.maximum(np.where(amax > 0, np.frexp(amax)[1] - 1 + 127, 0) - down, 1)
    scale = np.exp2(byte - 127.0)
    codes = (blocks / scale).astype(np.float32).astype(dtype).astype(np.float64)
    return np.moveaxis((codes * scale).reshape(v.shape), -1, axis)


WIDE = False


def mx_kscale(k):
    if not WIDE:
        return np.ones(k)
    levels = np.array([10, -10, 5, -5, 0])
    a = np.random.permutation(np.resize(levels, k // 512 * 4)).reshape(k // 512, 4)
    idx = np.arange(k)
    return np.exp2(a[idx // 512, idx % 128 // 32])


BF16 = ml_dtypes.bfloat16


def bf(x):
    return np.asarray(x, np.float32).astype(BF16)


def f64(x):
    return np.asarray(x).astype(np.float64)


B, IN, L = 256, 2048, 1536


def sigmoid(v):
    return 1.0 / (1.0 + np.exp(-v))


def setup_inputs():
    s = mx_kscale(IN)
    return {"input": bf(np.random.standard_normal((B, IN)) * s),
            "h0": bf(np.random.standard_normal((B, L))),
            "gh0": bf(np.random.standard_normal((B, 3 * L)) * 0.75),
            "W_ih0": bf(np.random.standard_normal((3 * L, IN)) * 0.7 / np.sqrt(IN) / s),
            "b_ih0": bf(np.random.standard_normal(3 * L) * 0.3)}


def reference(input, h0, gh0, W_ih0, b_ih0):
    h, gh = f64(h0), f64(gh0)
    gi = (mxq(f64(input), 1, "e4m3") @ mxq(f64(W_ih0), 1, "e4m3").T) + f64(b_ih0)
    i_r, i_z, i_n = gi[:, :L], gi[:, L:2 * L], gi[:, 2 * L:]
    h_r, h_z, h_n = gh[:, :L], gh[:, L:2 * L], gh[:, 2 * L:]
    r = sigmoid(i_r + h_r)
    z = sigmoid(i_z + h_z)
    n = np.tanh(i_n + r * h_n)
    return (1.0 - z) * n + z * h

@@ -1,0 +1,225 @@
+from contextlib import ExitStack
+
+import concourse.mybir as mybir
+from concourse.masks import make_identity
+
+F32 = mybir.dt.float32
+BF16 = mybir.dt.bfloat16
+U32 = mybir.dt.uint32
+U8 = mybir.dt.uint8
+FP8X4 = mybir.dt.float8_e4m3fn_x4
+ACT = mybir.ActivationFunctionType
+ALU = mybir.AluOpType
+
+P = 128
+BATCH, IN, L = 256, 2048, 1536
+FLOPS = 2 * BATCH * IN * 3 * L
+COLS = 256
+STEPS = 3 * L // COLS
+PASSES = IN // 512
+RING = 12
+GH_AFTER = {2: 0, 6: 1, 12: 2}
+H_AFTER = {4: 0, 7: 1, 13: 2}
+
+
+def tile_grucellstack_pa_kernel(tc, x_in, h0, gh0, w_ih0, b_ih0, out):
+    nc = tc.nc
+    with ExitStack() as ctx:
+        const = ctx.enter_context(tc.tile_pool(name="const", bufs=1))
+        rawp = ctx.enter_context(tc.tile_pool(name="rawp", bufs=RING))
+        grpp = ctx.enter_context(tc.tile_pool(name="grpp", bufs=3))
+        codp = ctx.enter_context(tc.tile_pool(name="codp", bufs=3))
+        ghbp = ctx.enter_context(tc.tile_pool(name="ghbp", bufs=2))
+        gatep = ctx.enter_context(tc.tile_pool(name="gatep", bufs=3))
+        outp = ctx.enter_context(tc.tile_pool(name="outp", bufs=6))
+        bankp = ctx.enter_context(tc.psum_pool(name="bankp", bufs=5))
+        accp = ctx.enter_context(tc.psum_pool(name="accp", bufs=3))
+
+        raw = {}
+        banks = {}
+        grouped = {}
+        codes = {}
+        scales = {}
+        acc = {}
+        gh_t = {}
+        h_t = {}
+        ghb = {}
+        t_r = {}
+        t_z = {}
+        z_h = {}
+
+        def load_rows(s):
+            raw[s] = rawp.tile([P, 2 * IN], BF16, name="raw", tag="raw")
+            if s < 0:
+                src = x_in
+            else:
+                row0 = (s % 3) * L + (s // 3) * COLS
+                src = w_ih0[row0 : row0 + COLS, :]
+            nc.sync.dma_start(out=raw[s][:], in_=src.rearrange("(p t) k -> p (t k)", t=2))
+            if s in GH_AFTER:
+                third = GH_AFTER[s]
+                gh_t[third] = const.tile([P, 2, 3, 512], BF16, name="gh%d" % third)
+                for b in range(2):
+                    nc.sync.dma_start(
+                        out=gh_t[third][:, b, :, :],
+                        in_=gh0[b * P : (b + 1) * P, :].rearrange("p (g c) -> p g c", g=3)[
+                            :, :, third * 512 : (third + 1) * 512
+                        ],
+                    )
+            if s in H_AFTER:
+                third = H_AFTER[s]
+                h_t[third] = const.tile([P, 2, 512], BF16, name="h%d" % third)
+                nc.sync.dma_start(
+                    out=h_t[third][:],
+                    in_=h0.rearrange("(b p) l -> p b l", p=P)[:, :, third * 512 : (third + 1) * 512],
+                )
+
+        def transposes(s, g):
+            bank = bankp.tile([P, 512], F32, name="bank", tag="bank")
+            words = raw[s][:].bitcast(F32)
+            for q in range(4):
+                t, u = q // 2, q % 2
+                col = t * (IN // 2) + g * 256 + u * P
+                nc.tensor.transpose(bank[:, q * P : (q + 1) * P], words[:, col : col + P], ident[:])
+            banks[(s, g)] = bank
+
+        def leave(s, g):
+            dst = grouped[s][:].bitcast(F32)[:, g * 512 : (g + 1) * 512]
+            nc.scalar.copy(
+                out=dst.rearrange("p (r q) -> p r q", q=4),
+                in_=banks[(s, g)][:].rearrange("p (q r) -> p r q", q=4),
+            )
+
+        def quantise(s):
+            if s < 0:
+                codes[s] = const.tile([P, PASSES * COLS], U32, name="xcodes", align_bytes=64)
+                scales[s] = const.tile([P, PASSES * COLS], U8, name="xscales", align_bytes=64)
+            else:
+                codes[s] = codp.tile([P, PASSES * COLS], U32, name="codes", tag="codes", align_bytes=64)
+                scales[s] = codp.tile([P, PASSES * COLS], U8, name="scales", tag="scales", align_bytes=64)
+            nc.vector.quantize_mx(out=codes[s][:].bitcast(FP8X4), scales=scales[s][:], in_=grouped[s][:])
+
+        def multiply(s):
+            acc[s] = accp.tile([P, 512], F32, name="acc", tag="acc")
+            for b in range(2):
+                for g in range(PASSES):
+                    xa = g * COLS + b * P
+                    nc.tensor.matmul_mx(
+                        out=acc[s][:, b * COLS : (b + 1) * COLS],
+                        lhsT=codes[-1][:, xa : xa + P].bitcast(FP8X4),
+                        lhsT_scale=scales[-1][:, xa : xa + P],
+                        rhs=codes[s][:, g * COLS : (g + 1) * COLS].bitcast(FP8X4),
+                        rhs_scale=scales[s][:, g * COLS : (g + 1) * COLS],
+                        start=(g == 0),
+                        stop=(g == PASSES - 1),
+                    )
+
+        def bias_block(i):
+            ps = accp.tile([P, 512], F32, name="bps", tag="acc")
+            nc.tensor.matmul(out=ps[:], lhsT=ones[:], rhs=bz[:, i * 512 : (i + 1) * 512], start=True, stop=True)
+            nc.vector.tensor_copy(out=bb[:, i * 512 : (i + 1) * 512], in_=ps[:])
+
+        def premerge(j):
+            third, o = j // 2, (j % 2) * COLS
+            ghb[j] = ghbp.tile([P, 2, 2, COLS], F32, name="ghb", tag="ghb")
+            bias2 = bb[:].rearrange("p (g c) -> p g c", g=3)[:, 0:2, j * COLS : (j + 1) * COLS]
+            nc.vector.tensor_tensor(
+                out=ghb[j][:],
+                in0=gh_t[third][:, :, 0:2, o : o + COLS],
+                in1=bias2.unsqueeze(1).to_broadcast([P, 2, 2, COLS]),
+                op=ALU.add,
+            )
+
+        def out_of_psum(s):
+            j, gate = s // 3, s % 3
+            sums = acc[s][:].rearrange("p (b c) -> p b c", b=2)
+            if gate == 0:
+                t_r[j] = gatep.tile([P, 2, COLS], F32, name="t_r", tag="t_r")
+                nc.vector.tensor_tensor(out=t_r[j][:], in0=sums, in1=ghb[j][:, :, 0, :], op=ALU.add)
+            elif gate == 1:
+                t_z[j] = gatep.tile([P, 2, COLS], F32, name="t_z", tag="t_z")
+                nc.vector.tensor_tensor(out=t_z[j][:], in0=sums, in1=ghb[j][:, :, 1, :], op=ALU.add)
+            else:
+                nc.vector.tensor_tensor(out=t_r[j][:], in0=sums, in1=t_r[j][:], op=ALU.add)
+
+        def activate(s):
+            j, gate = s // 3, s % 3
+            if gate == 0:
+                nc.scalar.activation(out=t_r[j][:], in_=t_r[j][:], func=ACT.Sigmoid)
+            elif gate == 1:
+                nc.scalar.activation(out=t_z[j][:], in_=t_z[j][:], func=ACT.Sigmoid)
+            else:
+                nc.scalar.activation(out=t_r[j][:], in_=t_r[j][:], func=ACT.Tanh)
+
+        def after(s):
+            j, gate = s // 3, s % 3
+            third, o = j // 2, (j % 2) * COLS
+            if gate == 0:
+                nc.vector.tensor_tensor(
+                    out=t_r[j][:], in0=t_r[j][:], in1=gh_t[third][:, :, 2, o : o + COLS], op=ALU.mult
+                )
+                bias_n = bb[:, 2 * L + j * COLS : 2 * L + (j + 1) * COLS]
+                nc.vector.tensor_tensor(
+                    out=t_r[j][:], in0=t_r[j][:], in1=bias_n.unsqueeze(1).to_broadcast([P, 2, COLS]), op=ALU.add
+                )
+            elif gate == 1:
+                z_h[j] = outp.tile([P, 2, COLS], F32, name="z_h", tag="z_h")
+                nc.vector.tensor_tensor(out=z_h[j][:], in0=t_z[j][:], in1=h_t[third][:, :, o : o + COLS], op=ALU.mult)
+            else:
+                nc.vector.scalar_tensor_tensor(
+                    out=t_z[j][:], in0=t_z[j][:], scalar=1.0, in1=t_r[j][:], op0=ALU.subtract, op1=ALU.mult
+                )
+                nc.vector.tensor_tensor(out=z_h[j][:], in0=z_h[j][:], in1=t_z[j][:], op=ALU.subtract)
+                nc.sync.dma_start(
+                    out=out.rearrange("(b p) l -> p b l", p=P)[:, :, j * COLS : (j + 1) * COLS], in_=z_h[j][:]
+                )
+
+        bz = const.tile([P, 3 * L], BF16, name="bz")
+        bb = const.tile([P, 3 * L], BF16, name="bb")
+        ones = const.tile([P, P], BF16, name="ones")
+        ident = const.tile([P, P], F32, name="ident")
+        warm = const.tile([P, 1], F32, name="warm")
+        nc.vector.memset(bz[:], 0.0)
+        nc.gpsimd.memset(warm[:], 0.0)
+        make_identity(nc, ident[:])
+        nc.gpsimd.memset(ones[:], 1.0)
+        ctx.enter_context(tc.manual_schedule())
+        nc.scalar.activation(out=warm[:], in_=warm[:], func=ACT.Sigmoid)
+        nc.scalar.dma_start(out=bz[0:1, :], in_=b_ih0.rearrange("(o n) -> o n", o=1))
+        for s in range(-1, RING - 1):
+            load_rows(s)
+
+        for g in range(PASSES):
+            transposes(-1, g)
+        load_rows(RING - 1)
+        for i in (0, 3, 6):
+            bias_block(i)
+
+        for m in range(-1, STEPS + 3):
+            if m < STEPS:
+                grouped[m] = grpp.tile([P, 4 * PASSES * COLS], BF16, name="grouped", tag="grouped", align_bytes=64)
+                for g in range(PASSES):
+                    leave(m, g)
+                    if m + 1 < STEPS:
+                        transposes(m + 1, g)
+                if m + 1 + RING < STEPS:
+                    load_rows(m + 1 + RING)
+            if -1 <= m - 1 < STEPS:
+                quantise(m - 1)
+            if m == -1:
+                for i in (1, 4, 7):
+                    bias_block(i)
+            if m == 0:
+                for i in (2, 5, 8):
+                    bias_block(i)
+            if 0 <= m - 1 < STEPS:
+                multiply(m - 1)
+            if m == 2:
+                premerge(0)
+            if 0 <= m - 2 < STEPS:
+                out_of_psum(m - 2)
+                activate(m - 2)
+            if 0 <= m - 3 < STEPS:
+                after(m - 3)
+            if m % 3 == 1 and m > 1 and (m - 1) // 3 < STEPS // 3:
+                premerge((m - 1) // 3)

@@ -16,10 +16,9 @@ BATCH, IN, L = 256, 2048, 1536
 FLOPS = 2 * BATCH * IN * 3 * L
 COLS = 256
 STEPS = 3 * L // COLS
+BLOCKS = L // COLS
 PASSES = IN // 512
 RING = 12
-GH_AFTER = {2: 0, 6: 1, 12: 2}
-H_AFTER = {4: 0, 7: 1, 13: 2}
 
 
 def tile_grucellstack_pa_kernel(tc, x_in, h0, gh0, w_ih0, b_ih0, out):
@@ -29,7 +28,6 @@ def tile_grucellstack_pa_kernel(tc, x_in, h0, gh0, w_ih0, b_ih0, out):
         rawp = ctx.enter_context(tc.tile_pool(name="rawp", bufs=RING))
         grpp = ctx.enter_context(tc.tile_pool(name="grpp", bufs=3))
         codp = ctx.enter_context(tc.tile_pool(name="codp", bufs=3))
-        ghbp = ctx.enter_context(tc.tile_pool(name="ghbp", bufs=2))
         gatep = ctx.enter_context(tc.tile_pool(name="gatep", bufs=3))
         outp = ctx.enter_context(tc.tile_pool(name="outp", bufs=6))
         bankp = ctx.enter_context(tc.psum_pool(name="bankp", bufs=5))
@@ -41,42 +39,38 @@ def tile_grucellstack_pa_kernel(tc, x_in, h0, gh0, w_ih0, b_ih0, out):
         codes = {}
         scales = {}
         acc = {}
-        gh_t = {}
+        gn_t = {}
         h_t = {}
-        ghb = {}
+        bias_ps = {}
         t_r = {}
         t_z = {}
         z_h = {}
 
+        gh_rows = gh0.rearrange("(b p) n -> p b n", p=P)
+        h_rows = h0.rearrange("(b p) l -> p b l", p=P)
+        out_rows = out.rearrange("(b p) l -> p b l", p=P)
+
         def load_rows(s):
-            raw[s] = rawp.tile([P, 2 * IN], BF16, name="raw", tag="raw")
+            raw[s] = rawp.tile([P, 2, IN], BF16, name="raw", tag="raw")
             if s < 0:
                 src = x_in
             else:
                 row0 = (s % 3) * L + (s // 3) * COLS
                 src = w_ih0[row0 : row0 + COLS, :]
-            nc.sync.dma_start(out=raw[s][:], in_=src.rearrange("(p t) k -> p (t k)", t=2))
-            if s in GH_AFTER:
-                third = GH_AFTER[s]
-                gh_t[third] = const.tile([P, 2, 3, 512], BF16, name="gh%d" % third)
-                for b in range(2):
-                    nc.sync.dma_start(
-                        out=gh_t[third][:, b, :, :],
-                        in_=gh0[b * P : (b + 1) * P, :].rearrange("p (g c) -> p g c", g=3)[
-                            :, :, third * 512 : (third + 1) * 512
-                        ],
-                    )
-            if s in H_AFTER:
-                third = H_AFTER[s]
-                h_t[third] = const.tile([P, 2, 512], BF16, name="h%d" % third)
+            nc.sync.dma_start(out=raw[s][:], in_=src.rearrange("(t p) k -> p t k", p=P))
+            third = s // 6
+            if s % 6 == 3:
+                gn_t[third] = const.tile([P, 2, 512], BF16, name="gn%d" % third)
                 nc.sync.dma_start(
-                    out=h_t[third][:],
-                    in_=h0.rearrange("(b p) l -> p b l", p=P)[:, :, third * 512 : (third + 1) * 512],
+                    out=gn_t[third][:], in_=gh_rows[:, :, 2 * L + third * 512 : 2 * L + (third + 1) * 512]
                 )
+            if s % 6 == 4:
+                h_t[third] = const.tile([P, 2, 512], BF16, name="h%d" % third)
+                nc.sync.dma_start(out=h_t[third][:], in_=h_rows[:, :, third * 512 : (third + 1) * 512])
 
         def transposes(s, g):
             bank = bankp.tile([P, 512], F32, name="bank", tag="bank")
-            words = raw[s][:].bitcast(F32)
+            words = raw[s][:].rearrange("p t k -> p (t k)").bitcast(F32)
             for q in range(4):
                 t, u = q // 2, q % 2
                 col = t * (IN // 2) + g * 256 + u * P
@@ -86,8 +80,8 @@ def tile_grucellstack_pa_kernel(tc, x_in, h0, gh0, w_ih0, b_ih0, out):
         def leave(s, g):
             dst = grouped[s][:].bitcast(F32)[:, g * 512 : (g + 1) * 512]
             nc.scalar.copy(
-                out=dst.rearrange("p (r q) -> p r q", q=4),
-                in_=banks[(s, g)][:].rearrange("p (q r) -> p r q", q=4),
+                out=dst.rearrange("p (t r u) -> p t r u", t=2, u=2),
+                in_=banks[(s, g)][:].rearrange("p (t u r) -> p t r u", t=2, u=2),
             )
 
         def quantise(s):
@@ -115,84 +109,89 @@ def tile_grucellstack_pa_kernel(tc, x_in, h0, gh0, w_ih0, b_ih0, out):
                     )
 
         def bias_block(i):
+            gate, third = i // 3, i % 3
+            cols = slice(third * 512, (third + 1) * 512)
             ps = accp.tile([P, 512], F32, name="bps", tag="acc")
             nc.tensor.matmul(out=ps[:], lhsT=ones[:], rhs=bz[:, i * 512 : (i + 1) * 512], start=True, stop=True)
-            nc.vector.tensor_copy(out=bb[:, i * 512 : (i + 1) * 512], in_=ps[:])
-
-        def premerge(j):
-            third, o = j // 2, (j % 2) * COLS
-            ghb[j] = ghbp.tile([P, 2, 2, COLS], F32, name="ghb", tag="ghb")
-            bias2 = bb[:].rearrange("p (g c) -> p g c", g=3)[:, 0:2, j * COLS : (j + 1) * COLS]
-            nc.vector.tensor_tensor(
-                out=ghb[j][:],
-                in0=gh_t[third][:, :, 0:2, o : o + COLS],
-                in1=bias2.unsqueeze(1).to_broadcast([P, 2, 2, COLS]),
-                op=ALU.add,
-            )
+            if gate < 2:
+                nc.vector.tensor_tensor(
+                    out=ghb[gate][:, :, cols],
+                    in0=gh_t[gate][:, :, cols],
+                    in1=ps[:].unsqueeze(1).to_broadcast([P, 2, 512]),
+                    op=ALU.add,
+                )
+            else:
+                bias_ps[third] = ps
 
         def out_of_psum(s):
             j, gate = s // 3, s % 3
+            cols = slice(j * COLS, (j + 1) * COLS)
             sums = acc[s][:].rearrange("p (b c) -> p b c", b=2)
             if gate == 0:
                 t_r[j] = gatep.tile([P, 2, COLS], F32, name="t_r", tag="t_r")
-                nc.vector.tensor_tensor(out=t_r[j][:], in0=sums, in1=ghb[j][:, :, 0, :], op=ALU.add)
-            elif gate == 1:
-                t_z[j] = gatep.tile([P, 2, COLS], F32, name="t_z", tag="t_z")
-                nc.vector.tensor_tensor(out=t_z[j][:], in0=sums, in1=ghb[j][:, :, 1, :], op=ALU.add)
-            else:
-                nc.vector.tensor_tensor(out=t_r[j][:], in0=sums, in1=t_r[j][:], op=ALU.add)
-
-        def activate(s):
-            j, gate = s // 3, s % 3
-            if gate == 0:
+                nc.vector.tensor_tensor(out=t_r[j][:], in0=sums, in1=ghb[0][:, :, cols], op=ALU.add)
                 nc.scalar.activation(out=t_r[j][:], in_=t_r[j][:], func=ACT.Sigmoid)
             elif gate == 1:
+                t_z[j] = gatep.tile([P, 2, COLS], F32, name="t_z", tag="t_z")
+                nc.vector.tensor_tensor(out=t_z[j][:], in0=sums, in1=ghb[1][:, :, cols], op=ALU.add)
                 nc.scalar.activation(out=t_z[j][:], in_=t_z[j][:], func=ACT.Sigmoid)
             else:
+                nc.vector.tensor_tensor(out=t_r[j][:], in0=sums, in1=t_r[j][:], op=ALU.add)
                 nc.scalar.activation(out=t_r[j][:], in_=t_r[j][:], func=ACT.Tanh)
 
-        def after(s):
-            j, gate = s // 3, s % 3
-            third, o = j // 2, (j % 2) * COLS
-            if gate == 0:
-                nc.vector.tensor_tensor(
-                    out=t_r[j][:], in0=t_r[j][:], in1=gh_t[third][:, :, 2, o : o + COLS], op=ALU.mult
-                )
-                bias_n = bb[:, 2 * L + j * COLS : 2 * L + (j + 1) * COLS]
-                nc.vector.tensor_tensor(
-                    out=t_r[j][:], in0=t_r[j][:], in1=bias_n.unsqueeze(1).to_broadcast([P, 2, COLS]), op=ALU.add
-                )
-            elif gate == 1:
-                z_h[j] = outp.tile([P, 2, COLS], F32, name="z_h", tag="z_h")
-                nc.vector.tensor_tensor(out=z_h[j][:], in0=t_z[j][:], in1=h_t[third][:, :, o : o + COLS], op=ALU.mult)
-            else:
-                nc.vector.scalar_tensor_tensor(
-                    out=t_z[j][:], in0=t_z[j][:], scalar=1.0, in1=t_r[j][:], op0=ALU.subtract, op1=ALU.mult
-                )
-                nc.vector.tensor_tensor(out=z_h[j][:], in0=z_h[j][:], in1=t_z[j][:], op=ALU.subtract)
-                nc.sync.dma_start(
-                    out=out.rearrange("(b p) l -> p b l", p=P)[:, :, j * COLS : (j + 1) * COLS], in_=z_h[j][:]
-                )
+        def part(j):
+            return j // 2, slice((j % 2) * COLS, (j % 2 + 1) * COLS)
+
+        def reset_times_gh(j):
+            third, cols = part(j)
+            nc.vector.tensor_tensor(out=t_r[j][:], in0=t_r[j][:], in1=gn_t[third][:, :, cols], op=ALU.mult)
+
+        def add_bias_n(j):
+            bias_n = bbn[:, j * COLS : (j + 1) * COLS]
+            nc.vector.tensor_tensor(
+                out=t_r[j][:], in0=t_r[j][:], in1=bias_n.unsqueeze(1).to_broadcast([P, 2, COLS]), op=ALU.add
+            )
+
+        def update_times_h(j):
+            third, cols = part(j)
+            z_h[j] = outp.tile([P, 2, COLS], F32, name="z_h", tag="z_h")
+            nc.vector.tensor_tensor(out=z_h[j][:], in0=t_z[j][:], in1=h_t[third][:, :, cols], op=ALU.mult)
+
+        def update_times_n(j):
+            nc.vector.scalar_tensor_tensor(
+                out=t_z[j][:], in0=t_z[j][:], scalar=1.0, in1=t_r[j][:], op0=ALU.subtract, op1=ALU.mult
+            )
+
+        def blend_and_store(j):
+            nc.vector.tensor_tensor(out=z_h[j][:], in0=z_h[j][:], in1=t_z[j][:], op=ALU.subtract)
+            nc.sync.dma_start(out=out_rows[:, :, j * COLS : (j + 1) * COLS], in_=z_h[j][:])
 
         bz = const.tile([P, 3 * L], BF16, name="bz")
-        bb = const.tile([P, 3 * L], BF16, name="bb")
+        bbn = const.tile([P, L], BF16, name="bbn")
         ones = const.tile([P, P], BF16, name="ones")
         ident = const.tile([P, P], F32, name="ident")
         warm = const.tile([P, 1], F32, name="warm")
-        nc.vector.memset(bz[:], 0.0)
+        gh_t = [const.tile([P, 2, L], BF16, name="gh_r"), const.tile([P, 2, L], BF16, name="gh_z")]
+        ghb = [const.tile([P, 2, L], F32, name="ghb_r"), const.tile([P, 2, L], F32, name="ghb_z")]
+        nc.vector.memset(bz[:, 0 : 3 * L // 2], 0.0)
+        nc.gpsimd.memset(bz[:, 3 * L // 2 : 3 * L], 0.0)
+        nc.gpsimd.memset(ones[:], 1.0)
         nc.gpsimd.memset(warm[:], 0.0)
         make_identity(nc, ident[:])
-        nc.gpsimd.memset(ones[:], 1.0)
         ctx.enter_context(tc.manual_schedule())
-        nc.scalar.activation(out=warm[:], in_=warm[:], func=ACT.Sigmoid)
         nc.scalar.dma_start(out=bz[0:1, :], in_=b_ih0.rearrange("(o n) -> o n", o=1))
+        nc.scalar.activation(out=warm[:], in_=warm[:], func=ACT.Sigmoid)
+        for gate in range(2):
+            nc.sync.dma_start(out=gh_t[gate][:], in_=gh_rows[:, :, gate * L : (gate + 1) * L])
         for s in range(-1, RING - 1):
             load_rows(s)
 
+        for i in range(4):
+            bias_block(i)
         for g in range(PASSES):
             transposes(-1, g)
         load_rows(RING - 1)
-        for i in (0, 3, 6):
+        for i in range(4, 6):
             bias_block(i)
 
         for m in range(-1, STEPS + 3):
@@ -204,22 +203,35 @@ def tile_grucellstack_pa_kernel(tc, x_in, h0, gh0, w_ih0, b_ih0, out):
                         transposes(m + 1, g)
                 if m + 1 + RING < STEPS:
                     load_rows(m + 1 + RING)
+            if m == -1:
+                for i in range(6, 9):
+                    bias_block(i)
             if -1 <= m - 1 < STEPS:
                 quantise(m - 1)
-            if m == -1:
-                for i in (1, 4, 7):
-                    bias_block(i)
             if m == 0:
-                for i in (2, 5, 8):
-                    bias_block(i)
+                for third in range(3):
+                    nc.vector.tensor_copy(out=bbn[:, third * 512 : (third + 1) * 512], in_=bias_ps[third][:])
             if 0 <= m - 1 < STEPS:
                 multiply(m - 1)
-            if m == 2:
-                premerge(0)
-            if 0 <= m - 2 < STEPS:
-                out_of_psum(m - 2)
-                activate(m - 2)
-            if 0 <= m - 3 < STEPS:
-                after(m - 3)
-            if m % 3 == 1 and m > 1 and (m - 1) // 3 < STEPS // 3:
-                premerge((m - 1) // 3)
+            j = (m - 3) // 3
+            late = 0 <= j < BLOCKS
+            sums_ready = 0 <= m - 2 < STEPS
+            if m % 3 == 0:
+                if late:
+                    reset_times_gh(j)
+                if sums_ready:
+                    out_of_psum(m - 2)
+                if late:
+                    add_bias_n(j)
+            elif m % 3 == 1:
+                if sums_ready:
+                    out_of_psum(m - 2)
+                if late:
+                    update_times_h(j)
+            else:
+                if late:
+                    update_times_n(j)
+                if sums_ready:
+                    out_of_psum(m - 2)
+                if late:
+                    blend_and_store(j)

@@ -41,7 +41,6 @@ def tile_grucellstack_pa_kernel(tc, x_in, h0, gh0, w_ih0, b_ih0, out):
         acc = {}
         gn_t = {}
         h_t = {}
-        bias_ps = {}
         t_r = {}
         t_z = {}
         z_h = {}
@@ -111,8 +110,13 @@ def tile_grucellstack_pa_kernel(tc, x_in, h0, gh0, w_ih0, b_ih0, out):
         def bias_block(i):
             gate, third = i // 3, i % 3
             cols = slice(third * 512, (third + 1) * 512)
-            ps = accp.tile([P, 512], F32, name="bps", tag="acc")
-            nc.tensor.matmul(out=ps[:], lhsT=ones[:], rhs=bz[:, i * 512 : (i + 1) * 512], start=True, stop=True)
+            if gate < 2:
+                ps = accp.tile([P, 512], F32, name="bps", tag="acc")
+            else:
+                ps = bankp.tile([P, 512], F32, name="bpn", tag="bank")
+            nc.tensor.matmul(
+                out=ps[:], lhsT=ident_bf[:, i : i + 1].to_broadcast([P, P]), rhs=b_rows[:], start=True, stop=True
+            )
             if gate < 2:
                 nc.vector.tensor_tensor(
                     out=ghb[gate][:, :, cols],
@@ -121,7 +125,7 @@ def tile_grucellstack_pa_kernel(tc, x_in, h0, gh0, w_ih0, b_ih0, out):
                     op=ALU.add,
                 )
             else:
-                bias_ps[third] = ps
+                nc.scalar.copy(out=bbn[:, cols], in_=ps[:])
 
         def out_of_psum(s):
             j, gate = s // 3, s % 3
@@ -166,27 +170,26 @@ def tile_grucellstack_pa_kernel(tc, x_in, h0, gh0, w_ih0, b_ih0, out):
             nc.vector.tensor_tensor(out=z_h[j][:], in0=z_h[j][:], in1=t_z[j][:], op=ALU.subtract)
             nc.sync.dma_start(out=out_rows[:, :, j * COLS : (j + 1) * COLS], in_=z_h[j][:])
 
-        bz = const.tile([P, 3 * L], BF16, name="bz")
+        b_rows = const.tile([P, 512], BF16, name="b_rows")
         bbn = const.tile([P, L], BF16, name="bbn")
-        ones = const.tile([P, P], BF16, name="ones")
+        ident_bf = const.tile([P, P], BF16, name="ident_bf")
         ident = const.tile([P, P], F32, name="ident")
         warm = const.tile([P, 1], F32, name="warm")
         gh_t = [const.tile([P, 2, L], BF16, name="gh_r"), const.tile([P, 2, L], BF16, name="gh_z")]
         ghb = [const.tile([P, 2, L], F32, name="ghb_r"), const.tile([P, 2, L], F32, name="ghb_z")]
-        nc.vector.memset(bz[:, 0 : 3 * L // 2], 0.0)
-        nc.gpsimd.memset(bz[:, 3 * L // 2 : 3 * L], 0.0)
-        nc.gpsimd.memset(ones[:], 1.0)
+        nc.vector.memset(b_rows[:], 0.0)
         nc.gpsimd.memset(warm[:], 0.0)
+        make_identity(nc, ident_bf[:])
         make_identity(nc, ident[:])
         ctx.enter_context(tc.manual_schedule())
-        nc.scalar.dma_start(out=bz[0:1, :], in_=b_ih0.rearrange("(o n) -> o n", o=1))
+        nc.sync.dma_start(out=b_rows[0:9, :], in_=b_ih0.rearrange("(i n) -> i n", n=512))
         nc.scalar.activation(out=warm[:], in_=warm[:], func=ACT.Sigmoid)
         for gate in range(2):
             nc.sync.dma_start(out=gh_t[gate][:], in_=gh_rows[:, :, gate * L : (gate + 1) * L])
         for s in range(-1, RING - 1):
             load_rows(s)
 
-        for i in range(4):
+        for i in (0, 1, 2, 6, 7, 8, 3):
             bias_block(i)
         for g in range(PASSES):
             transposes(-1, g)
@@ -203,14 +206,8 @@ def tile_grucellstack_pa_kernel(tc, x_in, h0, gh0, w_ih0, b_ih0, out):
                         transposes(m + 1, g)
                 if m + 1 + RING < STEPS:
                     load_rows(m + 1 + RING)
-            if m == -1:
-                for i in range(6, 9):
-                    bias_block(i)
             if -1 <= m - 1 < STEPS:
                 quantise(m - 1)
-            if m == 0:
-                for third in range(3):
-                    nc.vector.tensor_copy(out=bbn[:, third * 512 : (third + 1) * 512], in_=bias_ps[third][:])
             if 0 <= m - 1 < STEPS:
                 multiply(m - 1)
             j = (m - 3) // 3

@@ -78,10 +78,12 @@ def tile_grucellstack_pa_kernel(tc, x_in, h0, gh0, w_ih0, b_ih0, out):
 
         def leave(s, g):
             dst = grouped[s][:].bitcast(F32)[:, g * 512 : (g + 1) * 512]
-            nc.scalar.copy(
-                out=dst.rearrange("p (t r u) -> p t r u", t=2, u=2),
-                in_=banks[(s, g)][:].rearrange("p (t u r) -> p t r u", t=2, u=2),
-            )
+            dst = dst.rearrange("p (t r u) -> p t r u", t=2, u=2)
+            src = banks[(s, g)][:].rearrange("p (t u r) -> p t r u", t=2, u=2)
+            if s % 3 == 1 and g == 1:
+                nc.vector.tensor_copy(out=dst, in_=src)
+            else:
+                nc.scalar.copy(out=dst, in_=src)
 
         def quantise(s):
             if s < 0:

@@ -58,6 +58,8 @@ def tile_grucellstack_pa_kernel(tc, x_in, h0, gh0, w_ih0, b_ih0, out):
                 src = w_ih0[row0 : row0 + COLS, :]
             nc.sync.dma_start(out=raw[s][:], in_=src.rearrange("(t p) k -> p t k", p=P))
             third = s // 6
+            if s == 3:
+                nc.sync.dma_start(out=gh_t[1][:], in_=gh_rows[:, :, L : 2 * L])
             if s % 6 == 3:
                 gn_t[third] = const.tile([P, 2, 512], BF16, name="gn%d" % third)
                 nc.sync.dma_start(
@@ -78,12 +80,10 @@ def tile_grucellstack_pa_kernel(tc, x_in, h0, gh0, w_ih0, b_ih0, out):
 
         def leave(s, g):
             dst = grouped[s][:].bitcast(F32)[:, g * 512 : (g + 1) * 512]
-            dst = dst.rearrange("p (t r u) -> p t r u", t=2, u=2)
-            src = banks[(s, g)][:].rearrange("p (t u r) -> p t r u", t=2, u=2)
-            if s % 3 == 1 and g == 1:
-                nc.vector.tensor_copy(out=dst, in_=src)
-            else:
-                nc.scalar.copy(out=dst, in_=src)
+            nc.scalar.copy(
+                out=dst.rearrange("p (t r u) -> p t r u", t=2, u=2),
+                in_=banks[(s, g)][:].rearrange("p (t u r) -> p t r u", t=2, u=2),
+            )
 
         def quantise(s):
             if s < 0:
@@ -109,25 +109,31 @@ def tile_grucellstack_pa_kernel(tc, x_in, h0, gh0, w_ih0, b_ih0, out):
                         stop=(g == PASSES - 1),
                     )
 
-        def bias_block(i):
-            gate, third = i // 3, i % 3
-            cols = slice(third * 512, (third + 1) * 512)
-            if gate < 2:
-                ps = accp.tile([P, 512], F32, name="bps", tag="acc")
-            else:
-                ps = bankp.tile([P, 512], F32, name="bpn", tag="bank")
+        def spread_bias(gate, third):
+            i = 3 * gate + third
+            ps = accp.tile([P, 512], F32, name="bps", tag="acc")
             nc.tensor.matmul(
                 out=ps[:], lhsT=ident_bf[:, i : i + 1].to_broadcast([P, P]), rhs=b_rows[:], start=True, stop=True
             )
-            if gate < 2:
-                nc.vector.tensor_tensor(
-                    out=ghb[gate][:, :, cols],
-                    in0=gh_t[gate][:, :, cols],
-                    in1=ps[:].unsqueeze(1).to_broadcast([P, 2, 512]),
-                    op=ALU.add,
-                )
-            else:
-                nc.scalar.copy(out=bbn[:, cols], in_=ps[:])
+            return ps
+
+        def add_bias_r(third):
+            cols = slice(third * 512, (third + 1) * 512)
+            nc.vector.tensor_tensor(
+                out=ghb[0][:, :, cols],
+                in0=gh_t[0][:, :, cols],
+                in1=spread_bias(0, third)[:].unsqueeze(1).to_broadcast([P, 2, 512]),
+                op=ALU.add,
+            )
+
+        def add_bias_z(third):
+            cols = slice(third * 512, (third + 1) * 512)
+            nc.vector.tensor_tensor(
+                out=ghb[1][:, :, cols],
+                in0=gh_t[1][:, :, cols],
+                in1=bb[1][:, cols].unsqueeze(1).to_broadcast([P, 2, 512]),
+                op=ALU.add,
+            )
 
         def out_of_psum(s):
             j, gate = s // 3, s % 3
@@ -153,7 +159,7 @@ def tile_grucellstack_pa_kernel(tc, x_in, h0, gh0, w_ih0, b_ih0, out):
             nc.vector.tensor_tensor(out=t_r[j][:], in0=t_r[j][:], in1=gn_t[third][:, :, cols], op=ALU.mult)
 
         def add_bias_n(j):
-            bias_n = bbn[:, j * COLS : (j + 1) * COLS]
+            bias_n = bb[2][:, j * COLS : (j + 1) * COLS]
             nc.vector.tensor_tensor(
                 out=t_r[j][:], in0=t_r[j][:], in1=bias_n.unsqueeze(1).to_broadcast([P, 2, COLS]), op=ALU.add
             )
@@ -173,7 +179,7 @@ def tile_grucellstack_pa_kernel(tc, x_in, h0, gh0, w_ih0, b_ih0, out):
             nc.sync.dma_start(out=out_rows[:, :, j * COLS : (j + 1) * COLS], in_=z_h[j][:])
 
         b_rows = const.tile([P, 512], BF16, name="b_rows")
-        bbn = const.tile([P, L], BF16, name="bbn")
+        bb = {1: const.tile([P, L], BF16, name="bb_z"), 2: const.tile([P, L], BF16, name="bb_n")}
         ident_bf = const.tile([P, P], BF16, name="ident_bf")
         ident = const.tile([P, P], F32, name="ident")
         warm = const.tile([P, 1], F32, name="warm")
@@ -184,22 +190,21 @@ def tile_grucellstack_pa_kernel(tc, x_in, h0, gh0, w_ih0, b_ih0, out):
         make_identity(nc, ident_bf[:])
         make_identity(nc, ident[:])
         ctx.enter_context(tc.manual_schedule())
+        nc.sync.dma_start(out=gh_t[0][:], in_=gh_rows[:, :, 0:L])
         nc.sync.dma_start(out=b_rows[0:9, :], in_=b_ih0.rearrange("(i n) -> i n", n=512))
         nc.scalar.activation(out=warm[:], in_=warm[:], func=ACT.Sigmoid)
-        for gate in range(2):
-            nc.sync.dma_start(out=gh_t[gate][:], in_=gh_rows[:, :, gate * L : (gate + 1) * L])
         for s in range(-1, RING - 1):
             load_rows(s)
 
-        for i in (0, 1, 2, 6, 7, 8, 3):
-            bias_block(i)
+        for third in range(3):
+            add_bias_r(third)
         for g in range(PASSES):
             transposes(-1, g)
         load_rows(RING - 1)
-        for i in range(4, 6):
-            bias_block(i)
 
         for m in range(-1, STEPS + 3):
+            if m < 2:
+                spread = [(gate, spread_bias(gate, m + 1)) for gate in (1, 2)]
             if m < STEPS:
                 grouped[m] = grpp.tile([P, 4 * PASSES * COLS], BF16, name="grouped", tag="grouped", align_bytes=64)
                 for g in range(PASSES):
@@ -208,10 +213,15 @@ def tile_grucellstack_pa_kernel(tc, x_in, h0, gh0, w_ih0, b_ih0, out):
                         transposes(m + 1, g)
                 if m + 1 + RING < STEPS:
                     load_rows(m + 1 + RING)
+            if m < 2:
+                for gate, ps in spread:
+                    nc.scalar.copy(out=bb[gate][:, (m + 1) * 512 : (m + 2) * 512], in_=ps[:])
             if -1 <= m - 1 < STEPS:
                 quantise(m - 1)
             if 0 <= m - 1 < STEPS:
                 multiply(m - 1)
+            if 3 <= m < 6:
+                add_bias_z(m - 3)
             j = (m - 3) // 3
             late = 0 <= j < BLOCKS
             sums_ready = 0 <= m - 2 < STEPS

@@ -18,7 +18,24 @@ COLS = 256
 STEPS = 3 * L // COLS
 BLOCKS = L // COLS
 PASSES = IN // 512
-RING = 12
+RING = 11
+FIRST = ["r0", "z0"]
+SPREAD_PRE = {-2: ["r0", "z0"]}
+MPOS = 2
+MPOS_HEAD = 0
+HEAD = 4
+TBANKS = 5
+ABANKS = 2
+CHUNKED = 3
+POOL_ZH = False
+POOL_RG = False
+POOL_BIAS = False
+VCOPY = {}
+SPLIT_LAST = True
+ACT_POS = 4
+EXTRA = {0: ["r1", "z1"], 1: ["r2", "z2"], 2: ["n0"], 3: ["h0"], 6: ["n1"], 7: ["h1"], 12: ["n2"], 13: ["h2"]}
+SPREAD_AT = {-1: ["r1", "z1"], 0: ["r2", "z2"], 1: ["n0", "n1"], 6: ["n2"]}
+BIAS_AT = {"r0": -2, "z0": -2, "r1": 0, "z1": 0, "r2": 1, "z2": 1, "n0": 2, "n1": 2, "n2": 7}
 
 
 def tile_grucellstack_pa_kernel(tc, x_in, h0, gh0, w_ih0, b_ih0, out):
@@ -30,8 +47,9 @@ def tile_grucellstack_pa_kernel(tc, x_in, h0, gh0, w_ih0, b_ih0, out):
         codp = ctx.enter_context(tc.tile_pool(name="codp", bufs=3))
         gatep = ctx.enter_context(tc.tile_pool(name="gatep", bufs=3))
         outp = ctx.enter_context(tc.tile_pool(name="outp", bufs=6))
-        bankp = ctx.enter_context(tc.psum_pool(name="bankp", bufs=5))
-        accp = ctx.enter_context(tc.psum_pool(name="accp", bufs=3))
+        bankp = ctx.enter_context(tc.psum_pool(name="bankp", bufs=TBANKS))
+        accp = ctx.enter_context(tc.psum_pool(name="accp", bufs=ABANKS))
+        biasp = ctx.enter_context(tc.psum_pool(name="biasp", bufs=1))
 
         raw = {}
         banks = {}
@@ -39,8 +57,9 @@ def tile_grucellstack_pa_kernel(tc, x_in, h0, gh0, w_ih0, b_ih0, out):
         codes = {}
         scales = {}
         acc = {}
-        gn_t = {}
-        h_t = {}
+        gh_t = {}
+        ghb = {}
+        bb = {}
         t_r = {}
         t_z = {}
         z_h = {}
@@ -49,50 +68,91 @@ def tile_grucellstack_pa_kernel(tc, x_in, h0, gh0, w_ih0, b_ih0, out):
         h_rows = h0.rearrange("(b p) l -> p b l", p=P)
         out_rows = out.rearrange("(b p) l -> p b l", p=P)
 
-        def load_rows(s):
-            raw[s] = rawp.tile([P, 2, IN], BF16, name="raw", tag="raw")
+        def rows_of(s):
             if s < 0:
-                src = x_in
+                return x_in
+            row0 = (s % 3) * L + (s // 3) * COLS
+            return w_ih0[row0 : row0 + COLS, :]
+
+        def load_rows(s):
+            if s < CHUNKED:
+                if s < 0:
+                    raw[s] = const.tile([P, PASSES, 2, 512], BF16, name="xraw")
+                else:
+                    raw[s] = rawp.tile([P, PASSES, 2, 512], BF16, name="raw", tag="raw")
+                for g in range(PASSES):
+                    nc.sync.dma_start(
+                        out=raw[s][:, g, :, :], in_=rows_of(s)[:, g * 512 : (g + 1) * 512].rearrange("(t p) k -> p t k", p=P)
+                    )
             else:
-                row0 = (s % 3) * L + (s // 3) * COLS
-                src = w_ih0[row0 : row0 + COLS, :]
-            nc.sync.dma_start(out=raw[s][:], in_=src.rearrange("(t p) k -> p t k", p=P))
-            third = s // 6
-            if s == 3:
-                nc.sync.dma_start(out=gh_t[1][:], in_=gh_rows[:, :, L : 2 * L])
-            if s % 6 == 3:
-                gn_t[third] = const.tile([P, 2, 512], BF16, name="gn%d" % third)
-                nc.sync.dma_start(
-                    out=gn_t[third][:], in_=gh_rows[:, :, 2 * L + third * 512 : 2 * L + (third + 1) * 512]
-                )
-            if s % 6 == 4:
-                h_t[third] = const.tile([P, 2, 512], BF16, name="h%d" % third)
-                nc.sync.dma_start(out=h_t[third][:], in_=h_rows[:, :, third * 512 : (third + 1) * 512])
+                raw[s] = rawp.tile([P, 2, IN], BF16, name="raw", tag="raw")
+                nc.sync.dma_start(out=raw[s][:], in_=rows_of(s).rearrange("(t p) k -> p t k", p=P))
+            for what in EXTRA.get(s, []):
+                load_side(what)
+
+        def load_side(what):
+            kind, third = what[0], int(what[1])
+            gh_t[what] = const.tile([P, 2, 512], BF16, name="side_" + what)
+            if kind == "h":
+                src = h_rows[:, :, third * 512 : (third + 1) * 512]
+            else:
+                c0 = "rzn".index(kind) * L + third * 512
+                src = gh_rows[:, :, c0 : c0 + 512]
+            nc.sync.dma_start(out=gh_t[what][:], in_=src)
 
         def transposes(s, g):
             bank = bankp.tile([P, 512], F32, name="bank", tag="bank")
-            words = raw[s][:].rearrange("p t k -> p (t k)").bitcast(F32)
+            if s < CHUNKED:
+                words = raw[s][:].rearrange("p g t k -> p (g t k)").bitcast(F32)
+            else:
+                words = raw[s][:].rearrange("p t k -> p (t k)").bitcast(F32)
             for q in range(4):
                 t, u = q // 2, q % 2
-                col = t * (IN // 2) + g * 256 + u * P
+                if s < CHUNKED:
+                    col = g * 512 + t * 256 + u * P
+                else:
+                    col = t * (IN // 2) + g * 256 + u * P
                 nc.tensor.transpose(bank[:, q * P : (q + 1) * P], words[:, col : col + P], ident[:])
             banks[(s, g)] = bank
 
         def leave(s, g):
             dst = grouped[s][:].bitcast(F32)[:, g * 512 : (g + 1) * 512]
-            nc.scalar.copy(
-                out=dst.rearrange("p (t r u) -> p t r u", t=2, u=2),
-                in_=banks[(s, g)][:].rearrange("p (t u r) -> p t r u", t=2, u=2),
-            )
+            o = dst.rearrange("p (t r u) -> p t r u", t=2, u=2)
+            i = banks[(s, g)][:].rearrange("p (t u r) -> p t r u", t=2, u=2)
+            if (s, g) in VCOPY:
+                nc.vector.tensor_copy(out=o, in_=i)
+            else:
+                nc.scalar.copy(out=o, in_=i)
 
-        def quantise(s):
+        def new_codes(s):
             if s < 0:
                 codes[s] = const.tile([P, PASSES * COLS], U32, name="xcodes", align_bytes=64)
                 scales[s] = const.tile([P, PASSES * COLS], U8, name="xscales", align_bytes=64)
             else:
                 codes[s] = codp.tile([P, PASSES * COLS], U32, name="codes", tag="codes", align_bytes=64)
                 scales[s] = codp.tile([P, PASSES * COLS], U8, name="scales", tag="scales", align_bytes=64)
-            nc.vector.quantize_mx(out=codes[s][:].bitcast(FP8X4), scales=scales[s][:], in_=grouped[s][:])
+
+        def quantise(s, g0=0, g1=PASSES):
+            if g0 == 0:
+                new_codes(s)
+            nc.vector.quantize_mx(
+                out=codes[s][:, g0 * COLS : g1 * COLS].bitcast(FP8X4),
+                scales=scales[s][:, g0 * COLS : g1 * COLS],
+                in_=grouped[s][:, g0 * 4 * COLS : g1 * 4 * COLS],
+            )
+
+        def passes(s, b, g0, g1):
+            for g in range(g0, g1):
+                xa = g * COLS + b * P
+                nc.tensor.matmul_mx(
+                    out=acc[(s, b)][:, 0:COLS],
+                    lhsT=codes[-1][:, xa : xa + P].bitcast(FP8X4),
+                    lhsT_scale=scales[-1][:, xa : xa + P],
+                    rhs=codes[s][:, g * COLS : (g + 1) * COLS].bitcast(FP8X4),
+                    rhs_scale=scales[s][:, g * COLS : (g + 1) * COLS],
+                    start=(g == 0),
+                    stop=(g == PASSES - 1),
+                )
 
         def multiply(s):
             acc[s] = accp.tile([P, 512], F32, name="acc", tag="acc")
@@ -109,57 +169,71 @@ def tile_grucellstack_pa_kernel(tc, x_in, h0, gh0, w_ih0, b_ih0, out):
                         stop=(g == PASSES - 1),
                     )
 
-        def spread_bias(gate, third):
-            i = 3 * gate + third
-            ps = accp.tile([P, 512], F32, name="bps", tag="acc")
-            nc.tensor.matmul(
-                out=ps[:], lhsT=ident_bf[:, i : i + 1].to_broadcast([P, P]), rhs=b_rows[:], start=True, stop=True
-            )
-            return ps
+        def spread_bias(pair):
+            ps = biasp.tile([P, 1024], BF16, name="bias_bank", tag="bias_bank")
+            for slot, what in enumerate(pair):
+                i = 3 * "rzn".index(what[0]) + int(what[1])
+                nc.tensor.matmul(
+                    out=ps[:, slot * 512 : (slot + 1) * 512],
+                    lhsT=ident_bf[:, i : i + 1].to_broadcast([P, P]),
+                    rhs=b_rows[:],
+                    start=True,
+                    stop=True,
+                )
+                bb[what] = ps[:, slot * 512 : (slot + 1) * 512]
+            if POOL_BIAS and pair[0][0] != "n":
+                kept = const.tile([P, 1024], BF16, name="kept_" + pair[0])
+                nc.scalar.copy(out=kept[:], in_=ps[:])
+                for slot, what in enumerate(pair):
+                    bb[what] = kept[:, slot * 512 : (slot + 1) * 512]
 
-        def add_bias_r(third):
-            cols = slice(third * 512, (third + 1) * 512)
-            nc.vector.tensor_tensor(
-                out=ghb[0][:, :, cols],
-                in0=gh_t[0][:, :, cols],
-                in1=spread_bias(0, third)[:].unsqueeze(1).to_broadcast([P, 2, 512]),
+        def keep_bias_n(what):
+            third = int(what[1])
+            nc.scalar.copy(out=bb_n[:, third * 512 : (third + 1) * 512], in_=bb[what])
+
+        def add_bias(what):
+            kind, third = what[0], int(what[1])
+            ghb[what] = const.tile([P, 2, 512], F32, name="ghb_" + what)
+            eng = nc.gpsimd if POOL_BIAS else nc.vector
+            eng.tensor_tensor(
+                out=ghb[what][:],
+                in0=gh_t[what][:],
+                in1=bb[what].unsqueeze(1).to_broadcast([P, 2, 512]),
                 op=ALU.add,
             )
-
-        def add_bias_z(third):
-            cols = slice(third * 512, (third + 1) * 512)
-            nc.vector.tensor_tensor(
-                out=ghb[1][:, :, cols],
-                in0=gh_t[1][:, :, cols],
-                in1=bb[1][:, cols].unsqueeze(1).to_broadcast([P, 2, 512]),
-                op=ALU.add,
-            )
-
-        def out_of_psum(s):
-            j, gate = s // 3, s % 3
-            cols = slice(j * COLS, (j + 1) * COLS)
-            sums = acc[s][:].rearrange("p (b c) -> p b c", b=2)
-            if gate == 0:
-                t_r[j] = gatep.tile([P, 2, COLS], F32, name="t_r", tag="t_r")
-                nc.vector.tensor_tensor(out=t_r[j][:], in0=sums, in1=ghb[0][:, :, cols], op=ALU.add)
-                nc.scalar.activation(out=t_r[j][:], in_=t_r[j][:], func=ACT.Sigmoid)
-            elif gate == 1:
-                t_z[j] = gatep.tile([P, 2, COLS], F32, name="t_z", tag="t_z")
-                nc.vector.tensor_tensor(out=t_z[j][:], in0=sums, in1=ghb[1][:, :, cols], op=ALU.add)
-                nc.scalar.activation(out=t_z[j][:], in_=t_z[j][:], func=ACT.Sigmoid)
-            else:
-                nc.vector.tensor_tensor(out=t_r[j][:], in0=sums, in1=t_r[j][:], op=ALU.add)
-                nc.scalar.activation(out=t_r[j][:], in_=t_r[j][:], func=ACT.Tanh)
 
         def part(j):
             return j // 2, slice((j % 2) * COLS, (j % 2 + 1) * COLS)
 
+        def add_sums(s):
+            j, gate = s // 3, s % 3
+            third, cols = part(j)
+            sums = acc[s][:].rearrange("p (b c) -> p b c", b=2)
+            if gate == 0:
+                t_r[j] = gatep.tile([P, 2, COLS], F32, name="t_r", tag="t_r")
+                nc.vector.tensor_tensor(out=t_r[j][:], in0=sums, in1=ghb["r%d" % third][:, :, cols], op=ALU.add)
+            elif gate == 1:
+                t_z[j] = gatep.tile([P, 2, COLS], F32, name="t_z", tag="t_z")
+                nc.vector.tensor_tensor(out=t_z[j][:], in0=sums, in1=ghb["z%d" % third][:, :, cols], op=ALU.add)
+            else:
+                nc.vector.tensor_tensor(out=t_r[j][:], in0=sums, in1=t_r[j][:], op=ALU.add)
+
+        def activate(s):
+            j, gate = s // 3, s % 3
+            if gate == 0:
+                nc.scalar.activation(out=t_r[j][:], in_=t_r[j][:], func=ACT.Sigmoid)
+            elif gate == 1:
+                nc.scalar.activation(out=t_z[j][:], in_=t_z[j][:], func=ACT.Sigmoid)
+            else:
+                nc.scalar.activation(out=t_r[j][:], in_=t_r[j][:], func=ACT.Tanh)
+
         def reset_times_gh(j):
             third, cols = part(j)
-            nc.vector.tensor_tensor(out=t_r[j][:], in0=t_r[j][:], in1=gn_t[third][:, :, cols], op=ALU.mult)
+            eng = nc.gpsimd if POOL_RG else nc.vector
+            eng.tensor_tensor(out=t_r[j][:], in0=t_r[j][:], in1=gh_t["n%d" % third][:, :, cols], op=ALU.mult)
 
         def add_bias_n(j):
-            bias_n = bb[2][:, j * COLS : (j + 1) * COLS]
+            bias_n = bb_n[:, j * COLS : (j + 1) * COLS]
             nc.vector.tensor_tensor(
                 out=t_r[j][:], in0=t_r[j][:], in1=bias_n.unsqueeze(1).to_broadcast([P, 2, COLS]), op=ALU.add
             )
@@ -167,7 +241,8 @@ def tile_grucellstack_pa_kernel(tc, x_in, h0, gh0, w_ih0, b_ih0, out):
         def update_times_h(j):
             third, cols = part(j)
             z_h[j] = outp.tile([P, 2, COLS], F32, name="z_h", tag="z_h")
-            nc.vector.tensor_tensor(out=z_h[j][:], in0=t_z[j][:], in1=h_t[third][:, :, cols], op=ALU.mult)
+            eng = nc.gpsimd if POOL_ZH else nc.vector
+            eng.tensor_tensor(out=z_h[j][:], in0=t_z[j][:], in1=gh_t["h%d" % third][:, :, cols], op=ALU.mult)
 
         def update_times_n(j):
             nc.vector.scalar_tensor_tensor(
@@ -178,69 +253,69 @@ def tile_grucellstack_pa_kernel(tc, x_in, h0, gh0, w_ih0, b_ih0, out):
             nc.vector.tensor_tensor(out=z_h[j][:], in0=z_h[j][:], in1=t_z[j][:], op=ALU.subtract)
             nc.sync.dma_start(out=out_rows[:, :, j * COLS : (j + 1) * COLS], in_=z_h[j][:])
 
-        b_rows = const.tile([P, 512], BF16, name="b_rows")
-        bb = {1: const.tile([P, L], BF16, name="bb_z"), 2: const.tile([P, L], BF16, name="bb_n")}
-        ident_bf = const.tile([P, P], BF16, name="ident_bf")
         ident = const.tile([P, P], F32, name="ident")
-        warm = const.tile([P, 1], F32, name="warm")
-        gh_t = [const.tile([P, 2, L], BF16, name="gh_r"), const.tile([P, 2, L], BF16, name="gh_z")]
-        ghb = [const.tile([P, 2, L], F32, name="ghb_r"), const.tile([P, 2, L], F32, name="ghb_z")]
+        b_rows = const.tile([P, 512], BF16, name="b_rows")
+        bb_n = const.tile([P, L], BF16, name="bb_n")
+        ident_bf = const.tile([P, P], BF16, name="ident_bf")
         nc.vector.memset(b_rows[:], 0.0)
+        warm = const.tile([P, 1], F32, name="warm")
         nc.gpsimd.memset(warm[:], 0.0)
-        make_identity(nc, ident_bf[:])
         make_identity(nc, ident[:])
+        make_identity(nc, ident_bf[:])
         ctx.enter_context(tc.manual_schedule())
-        nc.sync.dma_start(out=gh_t[0][:], in_=gh_rows[:, :, 0:L])
-        nc.sync.dma_start(out=b_rows[0:9, :], in_=b_ih0.rearrange("(i n) -> i n", n=512))
         nc.scalar.activation(out=warm[:], in_=warm[:], func=ACT.Sigmoid)
-        for s in range(-1, RING - 1):
+        for what in FIRST:
+            load_side(what)
+        nc.sync.dma_start(out=b_rows[0:9, :], in_=b_ih0.rearrange("(i n) -> i n", n=512))
+        for s in range(-1, RING):
             load_rows(s)
 
-        for third in range(3):
-            add_bias_r(third)
-        for g in range(PASSES):
-            transposes(-1, g)
-        load_rows(RING - 1)
-
-        for m in range(-1, STEPS + 3):
-            if m < 2:
-                spread = [(gate, spread_bias(gate, m + 1)) for gate in (1, 2)]
-            if m < STEPS:
-                grouped[m] = grpp.tile([P, 4 * PASSES * COLS], BF16, name="grouped", tag="grouped", align_bytes=64)
-                for g in range(PASSES):
-                    leave(m, g)
-                    if m + 1 < STEPS:
-                        transposes(m + 1, g)
-                if m + 1 + RING < STEPS:
-                    load_rows(m + 1 + RING)
-            if m < 2:
-                for gate, ps in spread:
-                    nc.scalar.copy(out=bb[gate][:, (m + 1) * 512 : (m + 2) * 512], in_=ps[:])
-            if -1 <= m - 1 < STEPS:
-                quantise(m - 1)
-            if 0 <= m - 1 < STEPS:
-                multiply(m - 1)
-            if 3 <= m < 6:
-                add_bias_z(m - 3)
+        for m in range(-2, STEPS + 3):
+            if m in SPREAD_PRE:
+                spread_bias(SPREAD_PRE[m])
             j = (m - 3) // 3
             late = 0 <= j < BLOCKS
             sums_ready = 0 <= m - 2 < STEPS
-            if m % 3 == 0:
-                if late:
-                    reset_times_gh(j)
-                if sums_ready:
-                    out_of_psum(m - 2)
-                if late:
-                    add_bias_n(j)
-            elif m % 3 == 1:
-                if sums_ready:
-                    out_of_psum(m - 2)
-                if late:
-                    update_times_h(j)
-            else:
-                if late:
-                    update_times_n(j)
-                if sums_ready:
-                    out_of_psum(m - 2)
-                if late:
-                    blend_and_store(j)
+            last = SPLIT_LAST and m == STEPS - 1
+            if -1 <= m < STEPS:
+                grouped[m] = grpp.tile([P, 4 * PASSES * COLS], BF16, name="grouped", tag="grouped", align_bytes=64)
+            if -1 <= m - 1 < STEPS and not (SPLIT_LAST and m - 1 == STEPS - 1):
+                quantise(m - 1)
+            if late and m % 3 == 0:
+                reset_times_gh(j)
+            if late and m % 3 == 2:
+                update_times_n(j)
+            if sums_ready:
+                add_sums(m - 2)
+            mpos = MPOS_HEAD if m < HEAD else MPOS
+            for g in range(PASSES):
+                if g == mpos and 0 <= m - 1 < STEPS:
+                    multiply(m - 1)
+                if g == ACT_POS and sums_ready:
+                    activate(m - 2)
+                if -1 <= m < STEPS:
+                    leave(m, g)
+                if m + 1 < STEPS:
+                    transposes(m + 1, g)
+                if last and g % 2 == 1:
+                    quantise(m, g - 1, g + 1)
+            if 0 <= m + 1 and m + 1 + RING < STEPS:
+                load_rows(m + 1 + RING)
+            if ACT_POS >= PASSES and sums_ready:
+                activate(m - 2)
+            if mpos >= PASSES and 0 <= m - 1 < STEPS:
+                multiply(m - 1)
+            for what, at in BIAS_AT.items():
+                if at == m:
+                    if what[0] == "n":
+                        keep_bias_n(what)
+                    else:
+                        add_bias(what)
+            if m % 3 == 0 and late:
+                add_bias_n(j)
+            if m % 3 == 1 and late:
+                update_times_h(j)
+            if m % 3 == 2 and late:
+                blend_and_store(j)
+            if m in SPREAD_AT:
+                spread_bias(SPREAD_AT[m])

@@ -21,8 +21,8 @@ PASSES = IN // 512
 RING = 11
 FIRST = ["r0", "z0"]
 SPREAD_PRE = {-2: ["r0", "z0"]}
-MPOS = 2
-MPOS_HEAD = 0
+MPOS = (2, 2)
+MPOS_HEAD = (0, 2)
 HEAD = 4
 TBANKS = 5
 ABANKS = 2
@@ -74,6 +74,11 @@ def tile_grucellstack_pa_kernel(tc, x_in, h0, gh0, w_ih0, b_ih0, out):
             row0 = (s % 3) * L + (s // 3) * COLS
             return w_ih0[row0 : row0 + COLS, :]
 
+        def by_partition(s, rows):
+            if s < 0:
+                return rows.rearrange("(t p) k -> p t k", p=P)
+            return rows.rearrange("(p t) k -> p t k", t=2)
+
         def load_rows(s):
             if s < CHUNKED:
                 if s < 0:
@@ -81,12 +86,10 @@ def tile_grucellstack_pa_kernel(tc, x_in, h0, gh0, w_ih0, b_ih0, out):
                 else:
                     raw[s] = rawp.tile([P, PASSES, 2, 512], BF16, name="raw", tag="raw")
                 for g in range(PASSES):
-                    nc.sync.dma_start(
-                        out=raw[s][:, g, :, :], in_=rows_of(s)[:, g * 512 : (g + 1) * 512].rearrange("(t p) k -> p t k", p=P)
-                    )
+                    nc.sync.dma_start(out=raw[s][:, g, :, :], in_=by_partition(s, rows_of(s)[:, g * 512 : (g + 1) * 512]))
             else:
                 raw[s] = rawp.tile([P, 2, IN], BF16, name="raw", tag="raw")
-                nc.sync.dma_start(out=raw[s][:], in_=rows_of(s).rearrange("(t p) k -> p t k", p=P))
+                nc.sync.dma_start(out=raw[s][:], in_=by_partition(s, rows_of(s)))
             for what in EXTRA.get(s, []):
                 load_side(what)
 
@@ -154,9 +157,10 @@ def tile_grucellstack_pa_kernel(tc, x_in, h0, gh0, w_ih0, b_ih0, out):
                     stop=(g == PASSES - 1),
                 )
 
-        def multiply(s):
-            acc[s] = accp.tile([P, 512], F32, name="acc", tag="acc")
-            for b in range(2):
+        def multiply(s, halves=(0, 1)):
+            if halves[0] == 0:
+                acc[s] = accp.tile([P, 512], F32, name="acc", tag="acc")
+            for b in halves:
                 for g in range(PASSES):
                     xa = g * COLS + b * P
                     nc.tensor.matmul_mx(
@@ -205,18 +209,21 @@ def tile_grucellstack_pa_kernel(tc, x_in, h0, gh0, w_ih0, b_ih0, out):
         def part(j):
             return j // 2, slice((j % 2) * COLS, (j % 2 + 1) * COLS)
 
+        def pairs(ap):
+            return ap.rearrange("p b (r t) -> p b r t", t=2)
+
         def add_sums(s):
             j, gate = s // 3, s % 3
             third, cols = part(j)
-            sums = acc[s][:].rearrange("p (b c) -> p b c", b=2)
+            sums = acc[s][:].rearrange("p (b t r) -> p b r t", b=2, t=2)
             if gate == 0:
                 t_r[j] = gatep.tile([P, 2, COLS], F32, name="t_r", tag="t_r")
-                nc.vector.tensor_tensor(out=t_r[j][:], in0=sums, in1=ghb["r%d" % third][:, :, cols], op=ALU.add)
+                nc.vector.tensor_tensor(out=pairs(t_r[j][:]), in0=sums, in1=pairs(ghb["r%d" % third][:, :, cols]), op=ALU.add)
             elif gate == 1:
                 t_z[j] = gatep.tile([P, 2, COLS], F32, name="t_z", tag="t_z")
-                nc.vector.tensor_tensor(out=t_z[j][:], in0=sums, in1=ghb["z%d" % third][:, :, cols], op=ALU.add)
+                nc.vector.tensor_tensor(out=pairs(t_z[j][:]), in0=sums, in1=pairs(ghb["z%d" % third][:, :, cols]), op=ALU.add)
             else:
-                nc.vector.tensor_tensor(out=t_r[j][:], in0=sums, in1=t_r[j][:], op=ALU.add)
+                nc.vector.tensor_tensor(out=pairs(t_r[j][:]), in0=sums, in1=pairs(t_r[j][:]), op=ALU.add)
 
         def activate(s):
             j, gate = s // 3, s % 3
@@ -289,8 +296,9 @@ def tile_grucellstack_pa_kernel(tc, x_in, h0, gh0, w_ih0, b_ih0, out):
                 add_sums(m - 2)
             mpos = MPOS_HEAD if m < HEAD else MPOS
             for g in range(PASSES):
-                if g == mpos and 0 <= m - 1 < STEPS:
-                    multiply(m - 1)
+                for b in range(2):
+                    if g == mpos[b] and 0 <= m - 1 < STEPS:
+                        multiply(m - 1, (b,))
                 if g == ACT_POS and sums_ready:
                     activate(m - 2)
                 if -1 <= m < STEPS:
@@ -303,8 +311,9 @@ def tile_grucellstack_pa_kernel(tc, x_in, h0, gh0, w_ih0, b_ih0, out):
                 load_rows(m + 1 + RING)
             if ACT_POS >= PASSES and sums_ready:
                 activate(m - 2)
-            if mpos >= PASSES and 0 <= m - 1 < STEPS:
-                multiply(m - 1)
+            for b in range(2):
+                if mpos[b] >= PASSES and 0 <= m - 1 < STEPS:
+                    multiply(m - 1, (b,))
             for what, at in BIAS_AT.items():
                 if at == m:
                     if what[0] == "n":

@@ -19,23 +19,25 @@ STEPS = 3 * L // COLS
 BLOCKS = L // COLS
 PASSES = IN // 512
 RING = 11
-FIRST = ["r0", "z0"]
-SPREAD_PRE = {-2: ["r0", "z0"]}
+FIRST = []
+SPREAD_PRE = {-2: ["n0", "n1"]}
 MPOS = (2, 2)
 MPOS_HEAD = (0, 2)
 HEAD = 4
 TBANKS = 5
 ABANKS = 2
-CHUNKED = 3
+CHUNKED = -1
 POOL_ZH = False
 POOL_RG = False
 POOL_BIAS = False
+POOL_BN = False
+POOL_BL = False
 VCOPY = {}
 SPLIT_LAST = True
 ACT_POS = 4
-EXTRA = {0: ["r1", "z1"], 1: ["r2", "z2"], 2: ["n0"], 3: ["h0"], 6: ["n1"], 7: ["h1"], 12: ["n2"], 13: ["h2"]}
-SPREAD_AT = {-1: ["r1", "z1"], 0: ["r2", "z2"], 1: ["n0", "n1"], 6: ["n2"]}
-BIAS_AT = {"r0": -2, "z0": -2, "r1": 0, "z1": 0, "r2": 1, "z2": 1, "n0": 2, "n1": 2, "n2": 7}
+EXTRA = {0: ["r0"], 1: ["z0"], 2: ["n0"], 3: ["h0"], 5: ["r1"], 6: ["z1"], 7: ["n1"], 8: ["h1"], 11: ["r2"], 12: ["z2"], 13: ["n2"], 14: ["h2"]}
+SPREAD_AT = {-1: ["n2"], 0: ["r0", "z0"], 5: ["r1", "z1"], 11: ["r2", "z2"]}
+BIAS_AT = {"n0": -1, "n1": -1, "n2": 0, "r0": 1, "z0": 2, "r1": 6, "z1": 7, "r2": 12, "z2": 13}
 
 
 def tile_grucellstack_pa_kernel(tc, x_in, h0, gh0, w_ih0, b_ih0, out):
@@ -241,7 +243,8 @@ def tile_grucellstack_pa_kernel(tc, x_in, h0, gh0, w_ih0, b_ih0, out):
 
         def add_bias_n(j):
             bias_n = bb_n[:, j * COLS : (j + 1) * COLS]
-            nc.vector.tensor_tensor(
+            eng = nc.gpsimd if POOL_BN else nc.vector
+            eng.tensor_tensor(
                 out=t_r[j][:], in0=t_r[j][:], in1=bias_n.unsqueeze(1).to_broadcast([P, 2, COLS]), op=ALU.add
             )
 
@@ -257,7 +260,8 @@ def tile_grucellstack_pa_kernel(tc, x_in, h0, gh0, w_ih0, b_ih0, out):
             )
 
         def blend_and_store(j):
-            nc.vector.tensor_tensor(out=z_h[j][:], in0=z_h[j][:], in1=t_z[j][:], op=ALU.subtract)
+            eng = nc.gpsimd if (POOL_BL and j < BLOCKS - 1) else nc.vector
+            eng.tensor_tensor(out=z_h[j][:], in0=z_h[j][:], in1=t_z[j][:], op=ALU.subtract)
             nc.sync.dma_start(out=out_rows[:, :, j * COLS : (j + 1) * COLS], in_=z_h[j][:])
 
         ident = const.tile([P, P], F32, name="ident")
@@ -273,9 +277,10 @@ def tile_grucellstack_pa_kernel(tc, x_in, h0, gh0, w_ih0, b_ih0, out):
         nc.scalar.activation(out=warm[:], in_=warm[:], func=ACT.Sigmoid)
         for what in FIRST:
             load_side(what)
-        nc.sync.dma_start(out=b_rows[0:9, :], in_=b_ih0.rearrange("(i n) -> i n", n=512))
         for s in range(-1, RING):
             load_rows(s)
+            if s == -1:
+                nc.sync.dma_start(out=b_rows[0:9, :], in_=b_ih0.rearrange("(i n) -> i n", n=512))
 
         for m in range(-2, STEPS + 3):
             if m in SPREAD_PRE:

@@ -19,25 +19,17 @@ STEPS = 3 * L // COLS
 BLOCKS = L // COLS
 PASSES = IN // 512
 RING = 11
-FIRST = []
-SPREAD_PRE = {-2: ["n0", "n1"]}
-MPOS = (2, 2)
-MPOS_HEAD = (0, 2)
-HEAD = 4
-TBANKS = 5
-ABANKS = 2
-CHUNKED = -1
 POOL_ZH = False
-POOL_RG = False
-POOL_BIAS = False
+POOL_RG = True
 POOL_BN = False
-POOL_BL = False
-VCOPY = {}
-SPLIT_LAST = True
-ACT_POS = 4
-EXTRA = {0: ["r0"], 1: ["z0"], 2: ["n0"], 3: ["h0"], 5: ["r1"], 6: ["z1"], 7: ["n1"], 8: ["h1"], 11: ["r2"], 12: ["z2"], 13: ["n2"], 14: ["h2"]}
-SPREAD_AT = {-1: ["n2"], 0: ["r0", "z0"], 5: ["r1", "z1"], 11: ["r2", "z2"]}
-BIAS_AT = {"n0": -1, "n1": -1, "n2": 0, "r0": 1, "z0": 2, "r1": 6, "z1": 7, "r2": 12, "z2": 13}
+HEAD = 4
+MPOS = 2
+MPOS_HEAD = 2
+SEQ = [("r", 0)] + [x for j in range(BLOCKS - 1) for x in (("z", j), ("r", j + 1), ("n", j))] + [("z", BLOCKS - 1), ("n", BLOCKS - 1)]
+EXTRA = {0: ["r0"], 1: ["z0"], 2: ["n0"], 3: ["h0"], 4: ["r1"], 6: ["n1"], 7: ["z1"], 8: ["h1"], 10: ["r2"], 12: ["n2"], 13: ["z2"], 14: ["h2"]}
+SPREAD_PRE = {-2: ["n0", "n1"]}
+SPREAD_AT = {-1: ["n2"], 0: ["r0", "z0"], 4: ["r1", "z1"], 10: ["r2", "z2"]}
+BIAS_AT = {"n0": -1, "n1": -1, "n2": 0, "r0": 1, "z0": 2, "r1": 5, "z1": 8, "r2": 11, "z2": 14}
 
 
 def tile_grucellstack_pa_kernel(tc, x_in, h0, gh0, w_ih0, b_ih0, out):
@@ -49,8 +41,8 @@ def tile_grucellstack_pa_kernel(tc, x_in, h0, gh0, w_ih0, b_ih0, out):
         codp = ctx.enter_context(tc.tile_pool(name="codp", bufs=3))
         gatep = ctx.enter_context(tc.tile_pool(name="gatep", bufs=3))
         outp = ctx.enter_context(tc.tile_pool(name="outp", bufs=6))
-        bankp = ctx.enter_context(tc.psum_pool(name="bankp", bufs=TBANKS))
-        accp = ctx.enter_context(tc.psum_pool(name="accp", bufs=ABANKS))
+        bankp = ctx.enter_context(tc.psum_pool(name="bankp", bufs=5))
+        accp = ctx.enter_context(tc.psum_pool(name="accp", bufs=2))
         biasp = ctx.enter_context(tc.psum_pool(name="biasp", bufs=1))
 
         raw = {}
@@ -59,7 +51,7 @@ def tile_grucellstack_pa_kernel(tc, x_in, h0, gh0, w_ih0, b_ih0, out):
         codes = {}
         scales = {}
         acc = {}
-        gh_t = {}
+        side = {}
         ghb = {}
         bb = {}
         t_r = {}
@@ -70,99 +62,61 @@ def tile_grucellstack_pa_kernel(tc, x_in, h0, gh0, w_ih0, b_ih0, out):
         h_rows = h0.rearrange("(b p) l -> p b l", p=P)
         out_rows = out.rearrange("(b p) l -> p b l", p=P)
 
-        def rows_of(s):
-            if s < 0:
-                return x_in
-            row0 = (s % 3) * L + (s // 3) * COLS
-            return w_ih0[row0 : row0 + COLS, :]
-
-        def by_partition(s, rows):
-            if s < 0:
-                return rows.rearrange("(t p) k -> p t k", p=P)
-            return rows.rearrange("(p t) k -> p t k", t=2)
-
         def load_rows(s):
-            if s < CHUNKED:
-                if s < 0:
-                    raw[s] = const.tile([P, PASSES, 2, 512], BF16, name="xraw")
-                else:
-                    raw[s] = rawp.tile([P, PASSES, 2, 512], BF16, name="raw", tag="raw")
-                for g in range(PASSES):
-                    nc.sync.dma_start(out=raw[s][:, g, :, :], in_=by_partition(s, rows_of(s)[:, g * 512 : (g + 1) * 512]))
+            if s < 0:
+                raw[s] = const.tile([P, 2, IN], BF16, name="xraw")
+                nc.sync.dma_start(out=raw[s][:], in_=x_in.rearrange("(t p) k -> p t k", p=P))
             else:
+                gate, j = SEQ[s]
+                row0 = "rzn".index(gate) * L + j * COLS
                 raw[s] = rawp.tile([P, 2, IN], BF16, name="raw", tag="raw")
-                nc.sync.dma_start(out=raw[s][:], in_=by_partition(s, rows_of(s)))
+                nc.sync.dma_start(out=raw[s][:], in_=w_ih0[row0 : row0 + COLS, :].rearrange("(p t) k -> p t k", t=2))
             for what in EXTRA.get(s, []):
                 load_side(what)
 
         def load_side(what):
             kind, third = what[0], int(what[1])
-            gh_t[what] = const.tile([P, 2, 512], BF16, name="side_" + what)
+            side[what] = const.tile([P, 2, 512], BF16, name="side_" + what)
             if kind == "h":
                 src = h_rows[:, :, third * 512 : (third + 1) * 512]
             else:
                 c0 = "rzn".index(kind) * L + third * 512
                 src = gh_rows[:, :, c0 : c0 + 512]
-            nc.sync.dma_start(out=gh_t[what][:], in_=src)
+            nc.sync.dma_start(out=side[what][:], in_=src)
 
         def transposes(s, g):
             bank = bankp.tile([P, 512], F32, name="bank", tag="bank")
-            if s < CHUNKED:
-                words = raw[s][:].rearrange("p g t k -> p (g t k)").bitcast(F32)
-            else:
-                words = raw[s][:].rearrange("p t k -> p (t k)").bitcast(F32)
+            words = raw[s][:].rearrange("p t k -> p (t k)").bitcast(F32)
             for q in range(4):
                 t, u = q // 2, q % 2
-                if s < CHUNKED:
-                    col = g * 512 + t * 256 + u * P
-                else:
-                    col = t * (IN // 2) + g * 256 + u * P
+                col = t * (IN // 2) + g * 256 + u * P
                 nc.tensor.transpose(bank[:, q * P : (q + 1) * P], words[:, col : col + P], ident[:])
             banks[(s, g)] = bank
 
         def leave(s, g):
             dst = grouped[s][:].bitcast(F32)[:, g * 512 : (g + 1) * 512]
-            o = dst.rearrange("p (t r u) -> p t r u", t=2, u=2)
-            i = banks[(s, g)][:].rearrange("p (t u r) -> p t r u", t=2, u=2)
-            if (s, g) in VCOPY:
-                nc.vector.tensor_copy(out=o, in_=i)
-            else:
-                nc.scalar.copy(out=o, in_=i)
-
-        def new_codes(s):
-            if s < 0:
-                codes[s] = const.tile([P, PASSES * COLS], U32, name="xcodes", align_bytes=64)
-                scales[s] = const.tile([P, PASSES * COLS], U8, name="xscales", align_bytes=64)
-            else:
-                codes[s] = codp.tile([P, PASSES * COLS], U32, name="codes", tag="codes", align_bytes=64)
-                scales[s] = codp.tile([P, PASSES * COLS], U8, name="scales", tag="scales", align_bytes=64)
+            nc.scalar.copy(
+                out=dst.rearrange("p (t r u) -> p t r u", t=2, u=2),
+                in_=banks[(s, g)][:].rearrange("p (t u r) -> p t r u", t=2, u=2),
+            )
 
         def quantise(s, g0=0, g1=PASSES):
             if g0 == 0:
-                new_codes(s)
+                if s < 0:
+                    codes[s] = const.tile([P, PASSES * COLS], U32, name="xcodes", align_bytes=64)
+                    scales[s] = const.tile([P, PASSES * COLS], U8, name="xscales", align_bytes=64)
+                else:
+                    codes[s] = codp.tile([P, PASSES * COLS], U32, name="codes", tag="codes", align_bytes=64)
+                    scales[s] = codp.tile([P, PASSES * COLS], U8, name="scales", tag="scales", align_bytes=64)
             nc.vector.quantize_mx(
                 out=codes[s][:, g0 * COLS : g1 * COLS].bitcast(FP8X4),
                 scales=scales[s][:, g0 * COLS : g1 * COLS],
                 in_=grouped[s][:, g0 * 4 * COLS : g1 * 4 * COLS],
             )
 
-        def passes(s, b, g0, g1):
-            for g in range(g0, g1):
-                xa = g * COLS + b * P
-                nc.tensor.matmul_mx(
-                    out=acc[(s, b)][:, 0:COLS],
-                    lhsT=codes[-1][:, xa : xa + P].bitcast(FP8X4),
-                    lhsT_scale=scales[-1][:, xa : xa + P],
-                    rhs=codes[s][:, g * COLS : (g + 1) * COLS].bitcast(FP8X4),
-                    rhs_scale=scales[s][:, g * COLS : (g + 1) * COLS],
-                    start=(g == 0),
-                    stop=(g == PASSES - 1),
-                )
-
-        def multiply(s, halves=(0, 1)):
-            if halves[0] == 0:
-                acc[s] = accp.tile([P, 512], F32, name="acc", tag="acc")
-            for b in halves:
+        def multiply(s):
+            acc[s] = accp.tile([P, 512], F32, name="acc", tag="acc")
+            for b in range(2):
                 for g in range(PASSES):
                     xa = g * COLS + b * P
                     nc.tensor.matmul_mx(
@@ -187,25 +141,15 @@ def tile_grucellstack_pa_kernel(tc, x_in, h0, gh0, w_ih0, b_ih0, out):
                     stop=True,
                 )
                 bb[what] = ps[:, slot * 512 : (slot + 1) * 512]
-            if POOL_BIAS and pair[0][0] != "n":
-                kept = const.tile([P, 1024], BF16, name="kept_" + pair[0])
-                nc.scalar.copy(out=kept[:], in_=ps[:])
-                for slot, what in enumerate(pair):
-                    bb[what] = kept[:, slot * 512 : (slot + 1) * 512]
 
         def keep_bias_n(what):
             third = int(what[1])
             nc.scalar.copy(out=bb_n[:, third * 512 : (third + 1) * 512], in_=bb[what])
 
         def add_bias(what):
-            kind, third = what[0], int(what[1])
             ghb[what] = const.tile([P, 2, 512], F32, name="ghb_" + what)
-            eng = nc.gpsimd if POOL_BIAS else nc.vector
-            eng.tensor_tensor(
-                out=ghb[what][:],
-                in0=gh_t[what][:],
-                in1=bb[what].unsqueeze(1).to_broadcast([P, 2, 512]),
-                op=ALU.add,
+            nc.vector.tensor_tensor(
+                out=ghb[what][:], in0=side[what][:], in1=bb[what].unsqueeze(1).to_broadcast([P, 2, 512]), op=ALU.add
             )
 
         def part(j):
@@ -215,23 +159,23 @@ def tile_grucellstack_pa_kernel(tc, x_in, h0, gh0, w_ih0, b_ih0, out):
             return ap.rearrange("p b (r t) -> p b r t", t=2)
 
         def add_sums(s):
-            j, gate = s // 3, s % 3
+            gate, j = SEQ[s]
             third, cols = part(j)
             sums = acc[s][:].rearrange("p (b t r) -> p b r t", b=2, t=2)
-            if gate == 0:
+            if gate == "r":
                 t_r[j] = gatep.tile([P, 2, COLS], F32, name="t_r", tag="t_r")
                 nc.vector.tensor_tensor(out=pairs(t_r[j][:]), in0=sums, in1=pairs(ghb["r%d" % third][:, :, cols]), op=ALU.add)
-            elif gate == 1:
+            elif gate == "z":
                 t_z[j] = gatep.tile([P, 2, COLS], F32, name="t_z", tag="t_z")
                 nc.vector.tensor_tensor(out=pairs(t_z[j][:]), in0=sums, in1=pairs(ghb["z%d" % third][:, :, cols]), op=ALU.add)
             else:
                 nc.vector.tensor_tensor(out=pairs(t_r[j][:]), in0=sums, in1=pairs(t_r[j][:]), op=ALU.add)
 
         def activate(s):
-            j, gate = s // 3, s % 3
-            if gate == 0:
+            gate, j = SEQ[s]
+            if gate == "r":
                 nc.scalar.activation(out=t_r[j][:], in_=t_r[j][:], func=ACT.Sigmoid)
-            elif gate == 1:
+            elif gate == "z":
                 nc.scalar.activation(out=t_z[j][:], in_=t_z[j][:], func=ACT.Sigmoid)
             else:
                 nc.scalar.activation(out=t_r[j][:], in_=t_r[j][:], func=ACT.Tanh)
@@ -239,20 +183,18 @@ def tile_grucellstack_pa_kernel(tc, x_in, h0, gh0, w_ih0, b_ih0, out):
         def reset_times_gh(j):
             third, cols = part(j)
             eng = nc.gpsimd if POOL_RG else nc.vector
-            eng.tensor_tensor(out=t_r[j][:], in0=t_r[j][:], in1=gh_t["n%d" % third][:, :, cols], op=ALU.mult)
+            eng.tensor_tensor(out=t_r[j][:], in0=t_r[j][:], in1=side["n%d" % third][:, :, cols], op=ALU.mult)
 
         def add_bias_n(j):
             bias_n = bb_n[:, j * COLS : (j + 1) * COLS]
             eng = nc.gpsimd if POOL_BN else nc.vector
-            eng.tensor_tensor(
-                out=t_r[j][:], in0=t_r[j][:], in1=bias_n.unsqueeze(1).to_broadcast([P, 2, COLS]), op=ALU.add
-            )
+            eng.tensor_tensor(out=t_r[j][:], in0=t_r[j][:], in1=bias_n.unsqueeze(1).to_broadcast([P, 2, COLS]), op=ALU.add)
 
         def update_times_h(j):
             third, cols = part(j)
             z_h[j] = outp.tile([P, 2, COLS], F32, name="z_h", tag="z_h")
             eng = nc.gpsimd if POOL_ZH else nc.vector
-            eng.tensor_tensor(out=z_h[j][:], in0=t_z[j][:], in1=gh_t["h%d" % third][:, :, cols], op=ALU.mult)
+            eng.tensor_tensor(out=z_h[j][:], in0=t_z[j][:], in1=side["h%d" % third][:, :, cols], op=ALU.mult)
 
         def update_times_n(j):
             nc.vector.scalar_tensor_tensor(
@@ -260,9 +202,11 @@ def tile_grucellstack_pa_kernel(tc, x_in, h0, gh0, w_ih0, b_ih0, out):
             )
 
         def blend_and_store(j):
-            eng = nc.gpsimd if (POOL_BL and j < BLOCKS - 1) else nc.vector
-            eng.tensor_tensor(out=z_h[j][:], in0=z_h[j][:], in1=t_z[j][:], op=ALU.subtract)
+            nc.vector.tensor_tensor(out=z_h[j][:], in0=z_h[j][:], in1=t_z[j][:], op=ALU.subtract)
             nc.sync.dma_start(out=out_rows[:, :, j * COLS : (j + 1) * COLS], in_=z_h[j][:])
+
+        def block(j):
+            return 0 <= j < BLOCKS
 
         ident = const.tile([P, P], F32, name="ident")
         b_rows = const.tile([P, 512], BF16, name="b_rows")
@@ -275,8 +219,6 @@ def tile_grucellstack_pa_kernel(tc, x_in, h0, gh0, w_ih0, b_ih0, out):
         make_identity(nc, ident_bf[:])
         ctx.enter_context(tc.manual_schedule())
         nc.scalar.activation(out=warm[:], in_=warm[:], func=ACT.Sigmoid)
-        for what in FIRST:
-            load_side(what)
         for s in range(-1, RING):
             load_rows(s)
             if s == -1:
@@ -286,26 +228,52 @@ def tile_grucellstack_pa_kernel(tc, x_in, h0, gh0, w_ih0, b_ih0, out):
             if m in SPREAD_PRE:
                 spread_bias(SPREAD_PRE[m])
             j = (m - 3) // 3
-            late = 0 <= j < BLOCKS
+            phase = m % 3
             sums_ready = 0 <= m - 2 < STEPS
-            last = SPLIT_LAST and m == STEPS - 1
+            last = m == STEPS - 1
             if -1 <= m < STEPS:
                 grouped[m] = grpp.tile([P, 4 * PASSES * COLS], BF16, name="grouped", tag="grouped", align_bytes=64)
-            if -1 <= m - 1 < STEPS and not (SPLIT_LAST and m - 1 == STEPS - 1):
+            if -1 <= m - 1 < STEPS - 1:
                 quantise(m - 1)
-            if late and m % 3 == 0:
-                reset_times_gh(j)
-            if late and m % 3 == 2:
-                update_times_n(j)
-            if sums_ready:
-                add_sums(m - 2)
+            if phase == 0:
+                if block(j - 1):
+                    update_times_n(j - 1)
+                if m == 3:
+                    reset_times_gh(0)
+                if sums_ready:
+                    add_sums(m - 2)
+                if j == BLOCKS - 1:
+                    add_bias_n(j)
+                if block(j - 1):
+                    blend_and_store(j - 1)
+            elif phase == 1:
+                if sums_ready and j < BLOCKS - 1:
+                    add_sums(m - 2)
+                if block(j) and j < BLOCKS - 1:
+                    add_bias_n(j)
+                if sums_ready and j == BLOCKS - 1:
+                    add_sums(m - 2)
+                if block(j):
+                    update_times_h(j)
+            else:
+                if j == BLOCKS - 1:
+                    update_times_n(j)
+                if sums_ready:
+                    add_sums(m - 2)
+                if block(j + 1) and m > 2:
+                    reset_times_gh(j + 1)
+                if j == BLOCKS - 1:
+                    blend_and_store(j)
+            for what, at in BIAS_AT.items():
+                if at == m:
+                    if what[0] == "n":
+                        keep_bias_n(what)
+                    else:
+                        add_bias(what)
             mpos = MPOS_HEAD if m < HEAD else MPOS
             for g in range(PASSES):
-                for b in range(2):
-                    if g == mpos[b] and 0 <= m - 1 < STEPS:
-                        multiply(m - 1, (b,))
-                if g == ACT_POS and sums_ready:
-                    activate(m - 2)
+                if g == mpos and 0 <= m - 1 < STEPS:
+                    multiply(m - 1)
                 if -1 <= m < STEPS:
                     leave(m, g)
                 if m + 1 < STEPS:
@@ -314,22 +282,7 @@ def tile_grucellstack_pa_kernel(tc, x_in, h0, gh0, w_ih0, b_ih0, out):
                     quantise(m, g - 1, g + 1)
             if 0 <= m + 1 and m + 1 + RING < STEPS:
                 load_rows(m + 1 + RING)
-            if ACT_POS >= PASSES and sums_ready:
+            if sums_ready:
                 activate(m - 2)
-            for b in range(2):
-                if mpos[b] >= PASSES and 0 <= m - 1 < STEPS:
-                    multiply(m - 1, (b,))
-            for what, at in BIAS_AT.items():
-                if at == m:
-                    if what[0] == "n":
-                        keep_bias_n(what)
-                    else:
-                        add_bias(what)
-            if m % 3 == 0 and late:
-                add_bias_n(j)
-            if m % 3 == 1 and late:
-                update_times_h(j)
-            if m % 3 == 2 and late:
-                blend_and_store(j)
             if m in SPREAD_AT:
                 spread_bias(SPREAD_AT[m])

@@ -19,17 +19,20 @@ STEPS = 3 * L // COLS
 BLOCKS = L // COLS
 PASSES = IN // 512
 RING = 11
-POOL_ZH = False
+POOL_ZH = True
 POOL_RG = True
 POOL_BN = False
 HEAD = 4
+POOL_SPLIT = False
+NB_PSUM = True
+N_SPREAD = {3: 0, 6: 1, 9: 2, 12: 3, 15: 4, 17: 5}
 MPOS = 2
 MPOS_HEAD = 2
 SEQ = [("r", 0)] + [x for j in range(BLOCKS - 1) for x in (("z", j), ("r", j + 1), ("n", j))] + [("z", BLOCKS - 1), ("n", BLOCKS - 1)]
 EXTRA = {0: ["r0"], 1: ["z0"], 2: ["n0"], 3: ["h0"], 4: ["r1"], 6: ["n1"], 7: ["z1"], 8: ["h1"], 10: ["r2"], 12: ["n2"], 13: ["z2"], 14: ["h2"]}
-SPREAD_PRE = {-2: ["n0", "n1"]}
-SPREAD_AT = {-1: ["n2"], 0: ["r0", "z0"], 4: ["r1", "z1"], 10: ["r2", "z2"]}
-BIAS_AT = {"n0": -1, "n1": -1, "n2": 0, "r0": 1, "z0": 2, "r1": 5, "z1": 8, "r2": 11, "z2": 14}
+SPREAD_PRE = {}
+SPREAD_AT = {0: ["r0", "z0"], 4: ["r1"], 7: ["z1"], 10: ["r2"], 13: ["z2"]}
+BIAS_AT = {"r0": 1, "z0": 2, "r1": 5, "z1": 8, "r2": 11, "z2": 14}
 
 
 def tile_grucellstack_pa_kernel(tc, x_in, h0, gh0, w_ih0, b_ih0, out):
@@ -142,6 +145,17 @@ def tile_grucellstack_pa_kernel(tc, x_in, h0, gh0, w_ih0, b_ih0, out):
                 )
                 bb[what] = ps[:, slot * 512 : (slot + 1) * 512]
 
+        def spread_n(j):
+            ps = biasp.tile([P, 1024], BF16, name="bias_bank", tag="bias_bank")
+            nc.tensor.matmul(
+                out=ps[:, 0:COLS],
+                lhsT=ident_bf[:, 6 + j // 2 : 7 + j // 2].to_broadcast([P, P]),
+                rhs=b_rows[:, (j % 2) * COLS : (j % 2 + 1) * COLS],
+                start=True,
+                stop=True,
+            )
+            bb[("n", j)] = ps[:, 0:COLS]
+
         def keep_bias_n(what):
             third = int(what[1])
             nc.scalar.copy(out=bb_n[:, third * 512 : (third + 1) * 512], in_=bb[what])
@@ -183,10 +197,14 @@ def tile_grucellstack_pa_kernel(tc, x_in, h0, gh0, w_ih0, b_ih0, out):
         def reset_times_gh(j):
             third, cols = part(j)
             eng = nc.gpsimd if POOL_RG else nc.vector
-            eng.tensor_tensor(out=t_r[j][:], in0=t_r[j][:], in1=side["n%d" % third][:, :, cols], op=ALU.mult)
+            if POOL_RG and POOL_SPLIT:
+                for b in range(2):
+                    eng.tensor_tensor(out=t_r[j][:, b, :], in0=t_r[j][:, b, :], in1=side["n%d" % third][:, b, cols], op=ALU.mult)
+            else:
+                eng.tensor_tensor(out=t_r[j][:], in0=t_r[j][:], in1=side["n%d" % third][:, :, cols], op=ALU.mult)
 
         def add_bias_n(j):
-            bias_n = bb_n[:, j * COLS : (j + 1) * COLS]
+            bias_n = bb[("n", j)] if NB_PSUM else bb_n[:, j * COLS : (j + 1) * COLS]
             eng = nc.gpsimd if POOL_BN else nc.vector
             eng.tensor_tensor(out=t_r[j][:], in0=t_r[j][:], in1=bias_n.unsqueeze(1).to_broadcast([P, 2, COLS]), op=ALU.add)
 
@@ -286,3 +304,5 @@ def tile_grucellstack_pa_kernel(tc, x_in, h0, gh0, w_ih0, b_ih0, out):
                 activate(m - 2)
             if m in SPREAD_AT:
                 spread_bias(SPREAD_AT[m])
+            if NB_PSUM and m in N_SPREAD:
+                spread_n(N_SPREAD[m])

from contextlib import ExitStack

import concourse.mybir as mybir
from concourse.masks import make_identity

F32 = mybir.dt.float32
BF16 = mybir.dt.bfloat16
U32 = mybir.dt.uint32
U8 = mybir.dt.uint8
FP8X4 = mybir.dt.float8_e4m3fn_x4
ACT = mybir.ActivationFunctionType
ALU = mybir.AluOpType

P = 128
BATCH, IN, L = 256, 2048, 1536
FLOPS = 2 * BATCH * IN * 3 * L
COLS = 256
STEPS = 3 * L // COLS
BLOCKS = L // COLS
PASSES = IN // 512
RING = 11
POOL_ZH = True
POOL_RG = True
POOL_BN = False
HEAD = 4
POOL_SPLIT = False
NB_PSUM = True
N_SPREAD = {3: 0, 6: 1, 9: 2, 12: 3, 15: 4, 17: 5}
MPOS = 2
MPOS_HEAD = 2
SEQ = [("r", 0)] + [x for j in range(BLOCKS - 1) for x in (("z", j), ("r", j + 1), ("n", j))] + [("z", BLOCKS - 1), ("n", BLOCKS - 1)]
EXTRA = {0: ["r0"], 1: ["z0"], 2: ["n0"], 3: ["h0"], 4: ["r1"], 6: ["n1"], 7: ["z1"], 8: ["h1"], 10: ["r2"], 12: ["n2"], 13: ["z2"], 14: ["h2"]}
SPREAD_PRE = {}
SPREAD_AT = {0: ["r0", "z0"], 4: ["r1"], 7: ["z1"], 10: ["r2"], 13: ["z2"]}
BIAS_AT = {"r0": 1, "z0": 2, "r1": 5, "z1": 8, "r2": 11, "z2": 14}


def tile_grucellstack_pa_kernel(tc, x_in, h0, gh0, w_ih0, b_ih0, out):
    nc = tc.nc
    with ExitStack() as ctx:
        const = ctx.enter_context(tc.tile_pool(name="const", bufs=1))
        rawp = ctx.enter_context(tc.tile_pool(name="rawp", bufs=RING))
        grpp = ctx.enter_context(tc.tile_pool(name="grpp", bufs=3))
        codp = ctx.enter_context(tc.tile_pool(name="codp", bufs=3))
        gatep = ctx.enter_context(tc.tile_pool(name="gatep", bufs=3))
        outp = ctx.enter_context(tc.tile_pool(name="outp", bufs=6))
        bankp = ctx.enter_context(tc.psum_pool(name="bankp", bufs=5))
        accp = ctx.enter_context(tc.psum_pool(name="accp", bufs=2))
        biasp = ctx.enter_context(tc.psum_pool(name="biasp", bufs=1))

        raw = {}
        banks = {}
        grouped = {}
        codes = {}
        scales = {}
        acc = {}
        side = {}
        ghb = {}
        bb = {}
        t_r = {}
        t_z = {}
        z_h = {}

        gh_rows = gh0.rearrange("(b p) n -> p b n", p=P)
        h_rows = h0.rearrange("(b p) l -> p b l", p=P)
        out_rows = out.rearrange("(b p) l -> p b l", p=P)

        def load_rows(s):
            if s < 0:
                raw[s] = const.tile([P, 2, IN], BF16, name="xraw")
                nc.sync.dma_start(out=raw[s][:], in_=x_in.rearrange("(t p) k -> p t k", p=P))
            else:
                gate, j = SEQ[s]
                row0 = "rzn".index(gate) * L + j * COLS
                raw[s] = rawp.tile([P, 2, IN], BF16, name="raw", tag="raw")
                nc.sync.dma_start(out=raw[s][:], in_=w_ih0[row0 : row0 + COLS, :].rearrange("(p t) k -> p t k", t=2))
            for what in EXTRA.get(s, []):
                load_side(what)

        def load_side(what):
            kind, third = what[0], int(what[1])
            side[what] = const.tile([P, 2, 512], BF16, name="side_" + what)
            if kind == "h":
                src = h_rows[:, :, third * 512 : (third + 1) * 512]
            else:
                c0 = "rzn".index(kind) * L + third * 512
                src = gh_rows[:, :, c0 : c0 + 512]
            nc.sync.dma_start(out=side[what][:], in_=src)

        def transposes(s, g):
            bank = bankp.tile([P, 512], F32, name="bank", tag="bank")
            words = raw[s][:].rearrange("p t k -> p (t k)").bitcast(F32)
            for q in range(4):
                t, u = q // 2, q % 2
                col = t * (IN // 2) + g * 256 + u * P
                nc.tensor.transpose(bank[:, q * P : (q + 1) * P], words[:, col : col + P], ident[:])
            banks[(s, g)] = bank

        def leave(s, g):
            dst = grouped[s][:].bitcast(F32)[:, g * 512 : (g + 1) * 512]
            nc.scalar.copy(
                out=dst.rearrange("p (t r u) -> p t r u", t=2, u=2),
                in_=banks[(s, g)][:].rearrange("p (t u r) -> p t r u", t=2, u=2),
            )

        def quantise(s, g0=0, g1=PASSES):
            if g0 == 0:
                if s < 0:
                    codes[s] = const.tile([P, PASSES * COLS], U32, name="xcodes", align_bytes=64)
                    scales[s] = const.tile([P, PASSES * COLS], U8, name="xscales", align_bytes=64)
                else:
                    codes[s] = codp.tile([P, PASSES * COLS], U32, name="codes", tag="codes", align_bytes=64)
                    scales[s] = codp.tile([P, PASSES * COLS], U8, name="scales", tag="scales", align_bytes=64)
            nc.vector.quantize_mx(
                out=codes[s][:, g0 * COLS : g1 * COLS].bitcast(FP8X4),
                scales=scales[s][:, g0 * COLS : g1 * COLS],
                in_=grouped[s][:, g0 * 4 * COLS : g1 * 4 * COLS],
            )

        def multiply(s):
            acc[s] = accp.tile([P, 512], F32, name="acc", tag="acc")
            for b in range(2):
                for g in range(PASSES):
                    xa = g * COLS + b * P
                    nc.tensor.matmul_mx(
                        out=acc[s][:, b * COLS : (b + 1) * COLS],
                        lhsT=codes[-1][:, xa : xa + P].bitcast(FP8X4),
                        lhsT_scale=scales[-1][:, xa : xa + P],
                        rhs=codes[s][:, g * COLS : (g + 1) * COLS].bitcast(FP8X4),
                        rhs_scale=scales[s][:, g * COLS : (g + 1) * COLS],
                        start=(g == 0),
                        stop=(g == PASSES - 1),
                    )

        def spread_bias(pair):
            ps = biasp.tile([P, 1024], BF16, name="bias_bank", tag="bias_bank")
            for slot, what in enumerate(pair):
                i = 3 * "rzn".index(what[0]) + int(what[1])
                nc.tensor.matmul(
                    out=ps[:, slot * 512 : (slot + 1) * 512],
                    lhsT=ident_bf[:, i : i + 1].to_broadcast([P, P]),
                    rhs=b_rows[:],
                    start=True,
                    stop=True,
                )
                bb[what] = ps[:, slot * 512 : (slot + 1) * 512]

        def spread_n(j):
            ps = biasp.tile([P, 1024], BF16, name="bias_bank", tag="bias_bank")
            nc.tensor.matmul(
                out=ps[:, 0:COLS],
                lhsT=ident_bf[:, 6 + j // 2 : 7 + j // 2].to_broadcast([P, P]),
                rhs=b_rows[:, (j % 2) * COLS : (j % 2 + 1) * COLS],
                start=True,
                stop=True,
            )
            bb[("n", j)] = ps[:, 0:COLS]

        def keep_bias_n(what):
            third = int(what[1])
            nc.scalar.copy(out=bb_n[:, third * 512 : (third + 1) * 512], in_=bb[what])

        def add_bias(what):
            ghb[what] = const.tile([P, 2, 512], F32, name="ghb_" + what)
            nc.vector.tensor_tensor(
                out=ghb[what][:], in0=side[what][:], in1=bb[what].unsqueeze(1).to_broadcast([P, 2, 512]), op=ALU.add
            )

        def part(j):
            return j // 2, slice((j % 2) * COLS, (j % 2 + 1) * COLS)

        def pairs(ap):
            return ap.rearrange("p b (r t) -> p b r t", t=2)

        def add_sums(s):
            gate, j = SEQ[s]
            third, cols = part(j)
            sums = acc[s][:].rearrange("p (b t r) -> p b r t", b=2, t=2)
            if gate == "r":
                t_r[j] = gatep.tile([P, 2, COLS], F32, name="t_r", tag="t_r")
                nc.vector.tensor_tensor(out=pairs(t_r[j][:]), in0=sums, in1=pairs(ghb["r%d" % third][:, :, cols]), op=ALU.add)
            elif gate == "z":
                t_z[j] = gatep.tile([P, 2, COLS], F32, name="t_z", tag="t_z")
                nc.vector.tensor_tensor(out=pairs(t_z[j][:]), in0=sums, in1=pairs(ghb["z%d" % third][:, :, cols]), op=ALU.add)
            else:
                nc.vector.tensor_tensor(out=pairs(t_r[j][:]), in0=sums, in1=pairs(t_r[j][:]), op=ALU.add)

        def activate(s):
            gate, j = SEQ[s]
            if gate == "r":
                nc.scalar.activation(out=t_r[j][:], in_=t_r[j][:], func=ACT.Sigmoid)
            elif gate == "z":
                nc.scalar.activation(out=t_z[j][:], in_=t_z[j][:], func=ACT.Sigmoid)
            else:
                nc.scalar.activation(out=t_r[j][:], in_=t_r[j][:], func=ACT.Tanh)

        def reset_times_gh(j):
            third, cols = part(j)
            eng = nc.gpsimd if POOL_RG else nc.vector
            if POOL_RG and POOL_SPLIT:
                for b in range(2):
                    eng.tensor_tensor(out=t_r[j][:, b, :], in0=t_r[j][:, b, :], in1=side["n%d" % third][:, b, cols], op=ALU.mult)
            else:
                eng.tensor_tensor(out=t_r[j][:], in0=t_r[j][:], in1=side["n%d" % third][:, :, cols], op=ALU.mult)

        def add_bias_n(j):
            bias_n = bb[("n", j)] if NB_PSUM else bb_n[:, j * COLS : (j + 1) * COLS]
            eng = nc.gpsimd if POOL_BN else nc.vector
            eng.tensor_tensor(out=t_r[j][:], in0=t_r[j][:], in1=bias_n.unsqueeze(1).to_broadcast([P, 2, COLS]), op=ALU.add)

        def update_times_h(j):
            third, cols = part(j)
            z_h[j] = outp.tile([P, 2, COLS], F32, name="z_h", tag="z_h")
            eng = nc.gpsimd if POOL_ZH else nc.vector
            eng.tensor_tensor(out=z_h[j][:], in0=t_z[j][:], in1=side["h%d" % third][:, :, cols], op=ALU.mult)

        def update_times_n(j):
            nc.vector.scalar_tensor_tensor(
                out=t_z[j][:], in0=t_z[j][:], scalar=1.0, in1=t_r[j][:], op0=ALU.subtract, op1=ALU.mult
            )

        def blend_and_store(j):
            nc.vector.tensor_tensor(out=z_h[j][:], in0=z_h[j][:], in1=t_z[j][:], op=ALU.subtract)
            nc.sync.dma_start(out=out_rows[:, :, j * COLS : (j + 1) * COLS], in_=z_h[j][:])

        def block(j):
            return 0 <= j < BLOCKS

        ident = const.tile([P, P], F32, name="ident")
        b_rows = const.tile([P, 512], BF16, name="b_rows")
        bb_n = const.tile([P, L], BF16, name="bb_n")
        ident_bf = const.tile([P, P], BF16, name="ident_bf")
        nc.vector.memset(b_rows[:], 0.0)
        warm = const.tile([P, 1], F32, name="warm")
        nc.gpsimd.memset(warm[:], 0.0)
        make_identity(nc, ident[:])
        make_identity(nc, ident_bf[:])
        ctx.enter_context(tc.manual_schedule())
        nc.scalar.activation(out=warm[:], in_=warm[:], func=ACT.Sigmoid)
        for s in range(-1, RING):
            load_rows(s)
            if s == -1:
                nc.sync.dma_start(out=b_rows[0:9, :], in_=b_ih0.rearrange("(i n) -> i n", n=512))

        for m in range(-2, STEPS + 3):
            if m in SPREAD_PRE:
                spread_bias(SPREAD_PRE[m])
            j = (m - 3) // 3
            phase = m % 3
            sums_ready = 0 <= m - 2 < STEPS
            last = m == STEPS - 1
            if -1 <= m < STEPS:
                grouped[m] = grpp.tile([P, 4 * PASSES * COLS], BF16, name="grouped", tag="grouped", align_bytes=64)
            if -1 <= m - 1 < STEPS - 1:
                quantise(m - 1)
            if phase == 0:
                if block(j - 1):
                    update_times_n(j - 1)
                if m == 3:
                    reset_times_gh(0)
                if sums_ready:
                    add_sums(m - 2)
                if j == BLOCKS - 1:
                    add_bias_n(j)
                if block(j - 1):
                    blend_and_store(j - 1)
            elif phase == 1:
                if sums_ready and j < BLOCKS - 1:
                    add_sums(m - 2)
                if block(j) and j < BLOCKS - 1:
                    add_bias_n(j)
                if sums_ready and j == BLOCKS - 1:
                    add_sums(m - 2)
                if block(j):
                    update_times_h(j)
            else:
                if j == BLOCKS - 1:
                    update_times_n(j)
                if sums_ready:
                    add_sums(m - 2)
                if block(j + 1) and m > 2:
                    reset_times_gh(j + 1)
                if j == BLOCKS - 1:
                    blend_and_store(j)
            for what, at in BIAS_AT.items():
                if at == m:
                    if what[0] == "n":
                        keep_bias_n(what)
                    else:
                        add_bias(what)
            mpos = MPOS_HEAD if m < HEAD else MPOS
            for g in range(PASSES):
                if g == mpos and 0 <= m - 1 < STEPS:
                    multiply(m - 1)
                if -1 <= m < STEPS:
                    leave(m, g)
                if m + 1 < STEPS:
                    transposes(m + 1, g)
                if last and g % 2 == 1:
                    quantise(m, g - 1, g + 1)
            if 0 <= m + 1 and m + 1 + RING < STEPS:
                load_rows(m + 1 + RING)
            if sums_ready:
                activate(m - 2)
            if m in SPREAD_AT:
                spread_bias(SPREAD_AT[m])
            if NB_PSUM and m in N_SPREAD:
                spread_n(N_SPREAD[m])
